import numpy as np
import ml_dtypes


def mxq(x, axis, fmt="e4m3"):
    dtype, down = {"e4m3": (ml_dtypes.float8_e4m3fn, 7), "e5m2": (ml_dtypes.float8_e5m2, 14)}[fmt]
    v = np.moveaxis(np.asarray(x, np.float32).astype(ml_dtypes.bfloat16).astype(np.float64), axis, -1)
    blocks = v.reshape(v.shape[:-1] + (-1, 32))
    amax = np.abs(blocks).max(-1, keepdims=True)
    byte = np.maximum(np.where(amax > 0, np.frexp(amax)[1] - 1 + 127, 0) - down, 1)
    scale = np.exp2(byte - 127.0)
    codes = (blocks / scale).astype(np.float32).astype(dtype).astype(np.float64)
    return np.moveaxis((codes * scale).reshape(v.shape), -1, axis)


WIDE = False


def mx_kscale(k):
    if not WIDE:
        return np.ones(k)
    levels = np.array([10, -10, 5, -5, 0])
    if k % 512:
        return np.exp2(np.random.permutation(np.resize(levels, k // 32))).repeat(32)
    a = np.empty((k // 512, 16))
    for p in range(k // 512):
        a[p, :8] = np.random.permutation(np.resize(levels, 8))
        for g in range(8):
            far = levels[np.abs(levels - a[p, g]) >= 10]
            a[p, g + 8] = far[np.random.randint(len(far))]
    return np.exp2(a.ravel()).repeat(32)


BF16 = ml_dtypes.bfloat16


def bf(x):
    return np.asarray(x, np.float32).astype(BF16)


def f64(x):
    return np.asarray(x).astype(np.float64)


N, IN_F, OUT_F = 4096, 512, 128
POW = 2


def setup_inputs():
    s = mx_kscale(IN_F)
    u = np.exp2(np.round(np.log2(mx_kscale(N)) / 2))
    return {"input": bf(np.random.standard_normal((N, IN_F)) * s / (u * u)[:, None]),
            "adj": bf(np.random.uniform(0.0, 1.0, (N, N)) * 1.5 / N ** 0.25 * u),
            "weight": bf(np.random.uniform(-1.0, 1.0, (IN_F, OUT_F)) * 1.7 / np.sqrt(IN_F) / s[:, None]),
            "bias": bf(np.random.standard_normal(OUT_F) * 0.3)}


def reference(input, adj, weight, bias):
    k_adj = f64(adj) ** POW
    support = mxq(f64(input), 1, "e4m3") @ mxq(f64(weight), 0, "e4m3")
    out = (mxq(k_adj, 1, "e4m3") @ mxq(support, 0, "e4m3")) + f64(bias)
    return np.where(out > 0, out, np.expm1(out))

@@ -1,0 +1,353 @@
+from contextlib import ExitStack
+
+import concourse.mybir as mybir
+from concourse.masks import make_identity
+
+F32 = mybir.dt.float32
+BF16 = mybir.dt.bfloat16
+U32 = mybir.dt.uint32
+U8 = mybir.dt.uint8
+FP8X4 = mybir.dt.float8_e4m3fn_x4
+ACT = mybir.ActivationFunctionType
+ALU = mybir.AluOpType
+
+P = 128
+NODES = 4096
+IN_F = 512
+OUT_F = 128
+TILES = NODES // P
+CHUNKS = 4
+A_BUFS = 12
+X_PIECES = (4, 2, 1, 1)
+END_CUTS = (0, 2048, 3072, 4096)
+FLOPS = 2 * NODES * IN_F * OUT_F + 2 * NODES * NODES * OUT_F
+
+
+COPIES = (3, 2, 3, 2, 3, 2, 3, 2, 3, 2, 3, 2, 3, 2, 3, 2, 3, 2, 3, 2, 3, 2, 3, 2, 3, 2, 3, 2, 2, 2, 2, 2)
+JOBS = (("x", 0), ("x", 1), ("x", 2), ("x", 3))
+
+
+def copies_of(i):
+    return COPIES[i]
+
+
+def tile_netgraphconvolution_t_kernel(tc, x, adj, weight, bias, out):
+    nc = tc.nc
+    with ExitStack() as ctx:
+        const = ctx.enter_context(tc.tile_pool(name="const", bufs=1))
+        a_pool = ctx.enter_context(tc.tile_pool(name="a_pool", bufs=A_BUFS))
+        raw_pool = ctx.enter_context(tc.tile_pool(name="raw_pool", bufs=3))
+        grp_pool = ctx.enter_context(tc.tile_pool(name="grp_pool", bufs=4))
+        q_pool = ctx.enter_context(tc.tile_pool(name="q_pool", bufs=4))
+        ep_pool = ctx.enter_context(tc.tile_pool(name="ep_pool", bufs=2))
+        tp_pool = ctx.enter_context(tc.psum_pool(name="tp_pool", bufs=6))
+        acc_pool = ctx.enter_context(tc.psum_pool(name="acc_pool", bufs=2))
+        ctx.enter_context(tc.manual_schedule())
+
+        x_view = x.rearrange("(n p s) k -> p n (s k)", n=8, p=P, s=4)
+        w_view = weight.rearrange("(q t) c -> q (t c)", q=P, t=4)
+        adj_view = adj.rearrange("(g p s) k -> g s p k", g=8, p=P, s=4)
+        out_view = out.rearrange("(g p s) f -> g p s f", g=8, p=P, s=4)
+
+        ident = const.tile([P, P], F32, name="ident")
+        make_identity(nc, ident[:])
+
+        warm = const.tile([P, 2], F32, name="warm")
+        nc.vector.memset(warm[:, 0:1], 0.0)
+        nc.scalar.activation(out=warm[:, 1:2], in_=warm[:, 0:1], func=ACT.Exp)
+
+        a_tiles = {}
+
+        def load_x(h):
+            t = a_pool.tile([P, 4096], BF16, name="a", tag="a")
+            pieces = X_PIECES[h]
+            if pieces == 1:
+                nc.sync.dma_start(
+                    out=t[:].rearrange("p (n k) -> p n k", n=2),
+                    in_=x_view[:, 2 * h : 2 * h + 2, :],
+                )
+            else:
+                width = 4096 // pieces
+                for j in range(pieces):
+                    lo = width * j
+                    nc.sync.dma_start(
+                        out=t[:, lo : lo + width],
+                        in_=x_view[:, 2 * h + lo // 2048, lo % 2048 : lo % 2048 + width],
+                    )
+            a_tiles[("x", h)] = t
+
+        def load_a(i):
+            if i >= TILES:
+                return
+            t = a_pool.tile([P, 4096], BF16, name="a", tag="a")
+            nc.sync.dma_start(out=t[:], in_=adj_view[i // 4, i % 4])
+            a_tiles[("a", i)] = t
+
+        banks = {}
+
+        def transposes(key):
+            words = a_tiles[key][:].bitcast(F32)
+            made = []
+            for b in range(4):
+                tp = tp_pool.tile([P, 2, 256], F32, name="tp", tag="tp")
+                for g in range(2):
+                    for u in range(2):
+                        col = 512 * b + 256 * g
+                        nc.tensor.transpose(
+                            tp[:, u, 128 * g : 128 * g + 128],
+                            words[:, col + u : col + 256 : 2],
+                            ident[:],
+                        )
+                made.append(tp)
+            banks[key] = made
+
+        def new_codes():
+            codes = q_pool.tile([P, 1024], U32, name="codes", tag="codes", align_bytes=64)
+            scales = q_pool.tile([P, 1024], U8, name="scales", tag="scales", align_bytes=64)
+            return codes, scales
+
+        def quantise(grp, codes, scales, lo, hi):
+            nc.vector.quantize_mx(
+                out=codes[:, lo // 4 : hi // 4].bitcast(FP8X4),
+                scales=scales[:, lo // 4 : hi // 4],
+                in_=grp[:, lo:hi],
+            )
+
+        def words_out(engine_copy, dst_f32, tp, b):
+            engine_copy(
+                out=dst_f32[:, 512 * b : 512 * b + 512].rearrange("p (c u) -> p c u", u=2),
+                in_=tp[:].rearrange("p u c -> p c u"),
+            )
+
+        w_raw = const.tile([P, 4, OUT_F], BF16, name="w_raw")
+        for h in range(CHUNKS):
+            load_x(h)
+            if h == 0:
+                nc.sync.dma_start(out=w_raw[:].rearrange("p t c -> p (t c)"), in_=w_view)
+        bias_bf = const.tile([P, OUT_F], BF16, name="bias_bf")
+        for i in range(A_BUFS - CHUNKS):
+            load_a(i)
+            if i == 1:
+                nc.sync.dma_start(out=bias_bf[:], in_=bias.partition_broadcast(P))
+
+        w_grp = const.tile([P, OUT_F, 4], BF16, name="w_grp", align_bytes=64)
+        w_codes = const.tile([P, OUT_F], U32, name="w_codes", align_bytes=64)
+        w_scales = const.tile([P, OUT_F], U8, name="w_scales", align_bytes=64)
+        nc.vector.tensor_copy(out=w_grp[:], in_=w_raw[:].rearrange("p t c -> p c t"))
+        nc.vector.quantize_mx(
+            out=w_codes[:].bitcast(FP8X4),
+            scales=w_scales[:],
+            in_=w_grp[:].rearrange("p c t -> p (c t)"),
+        )
+
+        sup_grp = const.tile([P, 8, OUT_F, 4], BF16, name="sup_grp", align_bytes=64)
+        sup_codes = const.tile([P, 1024], U32, name="sup_codes", align_bytes=64)
+        sup_scales = const.tile([P, 1024], U8, name="sup_scales", align_bytes=64)
+        x_grp = {}
+        x_q = {}
+        x_acc = {}
+
+        def x_out(h):
+            grp = grp_pool.tile([P, 4096], BF16, name="grp", tag="grp", align_bytes=64)
+            x_grp[h] = grp
+            dst = grp[:].bitcast(F32)
+            made = banks[("x", h)]
+            for b in range(3):
+                words_out(nc.scalar.copy, dst, made[b], b)
+            words_out(nc.vector.tensor_copy, dst, made[3], 3)
+
+        def x_quant(h):
+            x_q[h] = new_codes()
+            quantise(x_grp[h], x_q[h][0], x_q[h][1], 0, 4096)
+
+        def x_matmuls(h):
+            codes, scales = x_q[h]
+            made = []
+            for cc in range(2):
+                acc = acc_pool.tile([P, 4, OUT_F], F32, name="acc", tag="acc")
+                for t in range(4):
+                    col = 512 * cc + 128 * t
+                    nc.tensor.matmul_mx(
+                        out=acc[:, t, :],
+                        lhsT=codes[:, col : col + 128].bitcast(FP8X4),
+                        lhsT_scale=scales[:, col : col + 128],
+                        rhs=w_codes[:].bitcast(FP8X4),
+                        rhs_scale=w_scales[:],
+                        start=True,
+                        stop=True,
+                    )
+                made.append(acc)
+            x_acc[h] = made
+
+        def sup_out(h):
+            nc.scalar.copy(
+                out=sup_grp[:, 2 * h, :, :], in_=x_acc[h][0][:].rearrange("p t w -> p w t")
+            )
+            nc.vector.tensor_copy(
+                out=sup_grp[:, 2 * h + 1, :, :], in_=x_acc[h][1][:].rearrange("p t w -> p w t")
+            )
+
+        a_grp = {}
+        a_q = {}
+
+        def a_out(i):
+            grp = grp_pool.tile([P, 4096], BF16, name="grp", tag="grp", align_bytes=64)
+            raw = raw_pool.tile([P, 2048], F32, name="raw", tag="raw")
+            a_grp[i] = (grp, raw)
+            made = banks[("a", i)]
+            for b in range(4):
+                if b < copies_of(i):
+                    words_out(nc.scalar.copy, raw, made[b], b)
+                else:
+                    nc.scalar.activation(
+                        out=grp[:, 1024 * b : 1024 * b + 1024].rearrange(
+                            "p (c u e) -> p c u e", u=2, e=2
+                        ),
+                        in_=made[b][:].bitcast(BF16).rearrange("p u (c e) -> p c u e", e=2),
+                        func=ACT.Square,
+                    )
+
+        def a_square(i):
+            grp, raw = a_grp[i]
+            raw_bf = raw[:].bitcast(BF16)
+            hi = 1024 * copies_of(i)
+            if hi > 0:
+                nc.vector.tensor_tensor(
+                    out=grp[:, 0:hi], in0=raw_bf[:, 0:hi], in1=raw_bf[:, 0:hi], op=ALU.mult
+                )
+
+        def a_quant(i, lo=0, hi=4096):
+            if lo == 0:
+                a_q[i] = new_codes()
+            quantise(a_grp[i][0], a_q[i][0], a_q[i][1], lo, hi)
+
+        units = [[4 * g, 4 * g + 1, 4 * g + 2, 4 * g + 3] for g in range(7)] + [[28, 29, 30], [31]]
+        unit_of = {}
+        for n, rows in enumerate(units):
+            for i in rows:
+                unit_of[i] = n
+        unit_acc = {}
+        unit_ep = {}
+
+        def a_matmuls(i, g_lo=0, g_hi=8):
+            n = unit_of[i]
+            if i == units[n][0] and g_lo == 0:
+                unit_acc[n] = acc_pool.tile([P, 4, OUT_F], F32, name="acc", tag="acc")
+            acc = unit_acc[n]
+            codes, scales = a_q[i]
+            s = i - units[n][0]
+            for g in range(g_lo, g_hi):
+                cols = slice(128 * g, 128 * g + 128)
+                nc.tensor.matmul_mx(
+                    out=acc[:, s, :],
+                    lhsT=codes[:, cols].bitcast(FP8X4),
+                    lhsT_scale=scales[:, cols],
+                    rhs=sup_codes[:, cols].bitcast(FP8X4),
+                    rhs_scale=sup_scales[:, cols],
+                    start=(g == 0),
+                    stop=(g == 7),
+                )
+
+        bias_f = const.tile([P, OUT_F], F32, name="bias_f")
+
+        def ep_first(n):
+            k = len(units[n])
+            v = ep_pool.tile([P, 4, OUT_F], F32, name="v", tag="v")
+            m = ep_pool.tile([P, 4, OUT_F], F32, name="m", tag="m")
+            nc.vector.tensor_tensor(
+                out=v[:, 0:k, :],
+                in0=unit_acc[n][:, 0:k, :],
+                in1=bias_f[:].unsqueeze(1).to_broadcast([P, k, OUT_F]),
+                op=ALU.add,
+            )
+            nc.vector.tensor_scalar_min(out=m[:, 0:k, :], in0=v[:, 0:k, :], scalar1=0.0)
+            unit_ep[n] = (v, m)
+
+        def ep_exp(n):
+            k = len(units[n])
+            v, m = unit_ep[n]
+            e = ep_pool.tile([P, 4, OUT_F], F32, name="e", tag="e")
+            nc.scalar.activation(out=e[:, 0:k, :], in_=m[:, 0:k, :], func=ACT.Exp)
+            unit_ep[n] = (v, e)
+
+        def ep_last(n):
+            k = len(units[n])
+            v, e = unit_ep[n]
+            o = ep_pool.tile([P, 4, OUT_F], F32, name="o", tag="o")
+            nc.vector.scalar_tensor_tensor(
+                out=o[:, 0:k, :],
+                in0=e[:, 0:k, :],
+                scalar=-1.0,
+                in1=v[:, 0:k, :],
+                op0=ALU.add,
+                op1=ALU.max,
+            )
+            first = units[n][0]
+            s0 = first % 4
+            nc.sync.dma_start(out=out_view[first // 4][:, s0 : s0 + k, :], in_=o[:, 0:k, :])
+
+        transposes(("x", 0))
+        for h in range(CHUNKS):
+            load_a(A_BUFS - CHUNKS + h)
+            if h + 1 < CHUNKS:
+                transposes(("x", h + 1))
+            else:
+                transposes(("a", 0))
+                load_a(A_BUFS)
+            x_out(h)
+            if h > 0:
+                sup_out(h - 1)
+            x_quant(h)
+            x_matmuls(h)
+        transposes(("a", 1))
+        load_a(A_BUFS + 1)
+
+        first_at = {}
+        exp_at = {}
+        last_at = {}
+        for n, rows in enumerate(units[:-2]):
+            first_at[rows[-1] + 2] = n
+            exp_at[rows[-1] + 3] = n
+            last_at[rows[-1] + 3] = n
+
+        for i in range(TILES - 1):
+            if i + 2 < TILES:
+                transposes(("a", i + 2))
+                load_a(i + 2 + A_BUFS)
+            a_out(i)
+            if i in exp_at:
+                ep_exp(exp_at[i])
+            a_square(i)
+            if i == 0:
+                sup_out(CHUNKS - 1)
+                nc.vector.quantize_mx(
+                    out=sup_codes[:].bitcast(FP8X4),
+                    scales=sup_scales[:],
+                    in_=sup_grp[:].rearrange("p c w t -> p (c w t)"),
+                )
+            if i == 3:
+                nc.vector.tensor_copy(out=bias_f[:], in_=bias_bf[:])
+            if i >= 1:
+                a_quant(i - 1)
+                a_matmuls(i - 1)
+            if i in first_at:
+                ep_first(first_at[i])
+            if i in last_at:
+                ep_last(last_at[i])
+
+        last = TILES - 1
+        a_out(last)
+        a_quant(last - 1)
+        a_matmuls(last - 1)
+        a_square(last)
+        ep_first(len(units) - 2)
+        ep_exp(len(units) - 2)
+        cuts = END_CUTS
+        for c in range(len(cuts) - 1):
+            a_quant(last, cuts[c], cuts[c + 1])
+            a_matmuls(last, cuts[c] // 512, cuts[c + 1] // 512)
+            if c == 0:
+                ep_last(len(units) - 2)
+        ep_first(len(units) - 1)
+        ep_exp(len(units) - 1)
+        ep_last(len(units) - 1)

@@ -16,19 +16,18 @@ NODES = 4096
 IN_F = 512
 OUT_F = 128
 TILES = NODES // P
-CHUNKS = 4
 A_BUFS = 12
-X_PIECES = (4, 2, 1, 1)
-END_CUTS = (0, 2048, 3072, 4096)
+PRE = 6
+PRE_COLS = 512 * PRE
+PRE_HALF = PRE_COLS // 4
+BANK_ORDER = (3, 0, 1, 2)
+END_CUTS = ((3072, 4096), (0, 2048), (2048, 3072))
 FLOPS = 2 * NODES * IN_F * OUT_F + 2 * NODES * NODES * OUT_F
 
-
-COPIES = (3, 2, 3, 2, 3, 2, 3, 2, 3, 2, 3, 2, 3, 2, 3, 2, 3, 2, 3, 2, 3, 2, 3, 2, 3, 2, 3, 2, 2, 2, 2, 2)
-JOBS = (("x", 0), ("x", 1), ("x", 2), ("x", 3))
-
-
-def copies_of(i):
-    return COPIES[i]
+JOBS = (
+    [("a", 0), ("x", 0), ("a", 1), ("a", 2), ("x", 1), ("a", 3), ("a", 4), ("x", 2), ("a", 5), ("a", 6), ("x", 3)]
+    + [("a", i) for i in range(7, TILES)]
+)
 
 
 def tile_netgraphconvolution_t_kernel(tc, x, adj, weight, bias, out):
@@ -36,15 +35,15 @@ def tile_netgraphconvolution_t_kernel(tc, x, adj, weight, bias, out):
     with ExitStack() as ctx:
         const = ctx.enter_context(tc.tile_pool(name="const", bufs=1))
         a_pool = ctx.enter_context(tc.tile_pool(name="a_pool", bufs=A_BUFS))
-        raw_pool = ctx.enter_context(tc.tile_pool(name="raw_pool", bufs=3))
-        grp_pool = ctx.enter_context(tc.tile_pool(name="grp_pool", bufs=4))
-        q_pool = ctx.enter_context(tc.tile_pool(name="q_pool", bufs=4))
+        sq_pool = ctx.enter_context(tc.tile_pool(name="sq_pool", bufs=3))
+        grp_pool = ctx.enter_context(tc.tile_pool(name="grp_pool", bufs=3))
+        q_pool = ctx.enter_context(tc.tile_pool(name="q_pool", bufs=11))
         ep_pool = ctx.enter_context(tc.tile_pool(name="ep_pool", bufs=2))
         tp_pool = ctx.enter_context(tc.psum_pool(name="tp_pool", bufs=6))
         acc_pool = ctx.enter_context(tc.psum_pool(name="acc_pool", bufs=2))
         ctx.enter_context(tc.manual_schedule())
 
-        x_view = x.rearrange("(n p s) k -> p n (s k)", n=8, p=P, s=4)
+        x_view = x.rearrange("(h p s) k -> h p (s k)", h=4, p=P, s=8)
         w_view = weight.rearrange("(q t) c -> q (t c)", q=P, t=4)
         adj_view = adj.rearrange("(g p s) k -> g s p k", g=8, p=P, s=4)
         out_view = out.rearrange("(g p s) f -> g p s f", g=8, p=P, s=4)
@@ -56,121 +55,148 @@ def tile_netgraphconvolution_t_kernel(tc, x, adj, weight, bias, out):
         nc.vector.memset(warm[:, 0:1], 0.0)
         nc.scalar.activation(out=warm[:, 1:2], in_=warm[:, 0:1], func=ACT.Exp)
 
-        a_tiles = {}
+        raw = {}
 
-        def load_x(h):
-            t = a_pool.tile([P, 4096], BF16, name="a", tag="a")
-            pieces = X_PIECES[h]
-            if pieces == 1:
-                nc.sync.dma_start(
-                    out=t[:].rearrange("p (n k) -> p n k", n=2),
-                    in_=x_view[:, 2 * h : 2 * h + 2, :],
-                )
-            else:
-                width = 4096 // pieces
-                for j in range(pieces):
-                    lo = width * j
-                    nc.sync.dma_start(
-                        out=t[:, lo : lo + width],
-                        in_=x_view[:, 2 * h + lo // 2048, lo % 2048 : lo % 2048 + width],
-                    )
-            a_tiles[("x", h)] = t
-
-        def load_a(i):
-            if i >= TILES:
+        def load(j, order=(0,)):
+            if j >= len(JOBS):
                 return
+            kind, i = JOBS[j]
             t = a_pool.tile([P, 4096], BF16, name="a", tag="a")
-            nc.sync.dma_start(out=t[:], in_=adj_view[i // 4, i % 4])
-            a_tiles[("a", i)] = t
+            src = x_view[i] if kind == "x" else adj_view[i // 4, i % 4]
+            width = 4096 // len(order)
+            for c in order:
+                cols = slice(width * c, width * c + width)
+                nc.sync.dma_start(out=t[:, cols], in_=src[:, cols])
+            raw[JOBS[j]] = t
+
+        squared = {}
+
+        def pre_square(j, lo=0, hi=PRE):
+            if j >= len(JOBS) or JOBS[j][0] == "x":
+                return
+            key = JOBS[j]
+            if lo == 0:
+                squared[key] = sq_pool.tile([P, PRE_COLS], BF16, name="sq", tag="sq")
+            src = raw[key][:, 512 * lo : 512 * hi].rearrange("p (q u v) -> p u q v", u=2, v=4)
+            dst = squared[key][:].rearrange("p (u q v) -> p u q v", u=2, v=4)[:, :, 64 * lo : 64 * hi, :]
+            nc.vector.tensor_tensor(out=dst, in0=src, in1=src, op=ALU.mult)
 
         banks = {}
 
-        def transposes(key):
-            words = a_tiles[key][:].bitcast(F32)
-            made = []
-            for b in range(4):
-                tp = tp_pool.tile([P, 2, 256], F32, name="tp", tag="tp")
-                for g in range(2):
-                    for u in range(2):
-                        col = 512 * b + 256 * g
-                        nc.tensor.transpose(
-                            tp[:, u, 128 * g : 128 * g + 128],
-                            words[:, col + u : col + 256 : 2],
-                            ident[:],
-                        )
-                made.append(tp)
+        def transposes(j):
+            if j >= len(JOBS):
+                return
+            key = JOBS[j]
+            words = raw[key][:].bitcast(F32)
+            made = {}
+            for b in range(4) if key[0] == "x" else BANK_ORDER:
+                tp = tp_pool.tile([P, 4, P], F32, name="tp", tag="tp")
+                if key[0] == "x":
+                    for v in range(2):
+                        s = 4 * (b // 2) + b % 2 + 2 * v if key[1] < PRE // 2 else b + 4 * v
+                        for e in range(2):
+                            nc.tensor.transpose(
+                                tp[:, 2 * v + e, :],
+                                words[:, 256 * s + e : 256 * s + 256 : 2],
+                                ident[:],
+                            )
+                else:
+                    for g in range(2):
+                        n = 2 * b + g
+                        for u in range(2):
+                            if n < PRE:
+                                lo = PRE_HALF * u + 128 * n
+                                src = squared[key][:].bitcast(F32)[:, lo : lo + 128]
+                            else:
+                                src = words[:, 256 * n + u : 256 * n + 256 : 2]
+                            nc.tensor.transpose(tp[:, 2 * u + g, :], src, ident[:])
+                made[b] = tp
             banks[key] = made
 
-        def new_codes():
-            codes = q_pool.tile([P, 1024], U32, name="codes", tag="codes", align_bytes=64)
-            scales = q_pool.tile([P, 1024], U8, name="scales", tag="scales", align_bytes=64)
-            return codes, scales
-
-        def quantise(grp, codes, scales, lo, hi):
-            nc.vector.quantize_mx(
-                out=codes[:, lo // 4 : hi // 4].bitcast(FP8X4),
-                scales=scales[:, lo // 4 : hi // 4],
-                in_=grp[:, lo:hi],
-            )
-
-        def words_out(engine_copy, dst_f32, tp, b):
-            engine_copy(
-                out=dst_f32[:, 512 * b : 512 * b + 512].rearrange("p (c u) -> p c u", u=2),
-                in_=tp[:].rearrange("p u c -> p c u"),
-            )
-
         w_raw = const.tile([P, 4, OUT_F], BF16, name="w_raw")
-        for h in range(CHUNKS):
-            load_x(h)
-            if h == 0:
-                nc.sync.dma_start(out=w_raw[:].rearrange("p t c -> p (t c)"), in_=w_view)
         bias_bf = const.tile([P, OUT_F], BF16, name="bias_bf")
-        for i in range(A_BUFS - CHUNKS):
-            load_a(i)
-            if i == 1:
+        for j in range(A_BUFS):
+            load(j, ((3, 0, 1, 2), (0, 1), (1, 0))[j] if j < 3 else (0,))
+            if j == 1:
+                nc.sync.dma_start(out=w_raw[:].rearrange("p t c -> p (t c)"), in_=w_view)
+            if j == 7:
                 nc.sync.dma_start(out=bias_bf[:], in_=bias.partition_broadcast(P))
 
         w_grp = const.tile([P, OUT_F, 4], BF16, name="w_grp", align_bytes=64)
         w_codes = const.tile([P, OUT_F], U32, name="w_codes", align_bytes=64)
         w_scales = const.tile([P, OUT_F], U8, name="w_scales", align_bytes=64)
-        nc.vector.tensor_copy(out=w_grp[:], in_=w_raw[:].rearrange("p t c -> p c t"))
-        nc.vector.quantize_mx(
-            out=w_codes[:].bitcast(FP8X4),
-            scales=w_scales[:],
-            in_=w_grp[:].rearrange("p c t -> p (c t)"),
-        )
-
         sup_grp = const.tile([P, 8, OUT_F, 4], BF16, name="sup_grp", align_bytes=64)
         sup_codes = const.tile([P, 1024], U32, name="sup_codes", align_bytes=64)
         sup_scales = const.tile([P, 1024], U8, name="sup_scales", align_bytes=64)
-        x_grp = {}
-        x_q = {}
+        bias_f = const.tile([P, OUT_F], F32, name="bias_f")
+
+        def weight_out():
+            nc.vector.tensor_copy(out=w_grp[:], in_=w_raw[:].rearrange("p t c -> p c t"))
+
+        def weight_quant():
+            nc.vector.quantize_mx(
+                out=w_codes[:].bitcast(FP8X4),
+                scales=w_scales[:],
+                in_=w_grp[:].rearrange("p c t -> p (c t)"),
+            )
+
+        grp = {}
+        codes_of = {}
+
+        def evacuate(j, skip=(), copy=nc.scalar.copy):
+            key = JOBS[j]
+            if key not in grp:
+                grp[key] = grp_pool.tile([P, 4096], BF16, name="grp", tag="grp", align_bytes=64)
+            t = grp[key]
+            dst = t[:].bitcast(F32)
+            for b, tp in banks[key].items():
+                if b in skip:
+                    continue
+                if key[0] == "x":
+                    copy(
+                        out=dst.rearrange("p (c t q j) -> p t c q j", c=2, t=4, j=4)[:, b],
+                        in_=tp[:].rearrange("p j (c q) -> p c q j", c=2),
+                    )
+                elif 2 * b < PRE:
+                    copy(
+                        out=dst[:, 512 * b : 512 * b + 512].rearrange("p (c u) -> p c u", u=2),
+                        in_=tp[:].rearrange("p (u g) c -> p (g c) u", u=2),
+                    )
+                else:
+                    nc.scalar.activation(
+                        out=t[:, 1024 * b : 1024 * b + 1024].rearrange("p (c u e) -> p c u e", u=2, e=2),
+                        in_=tp[:].rearrange("p (u g) c -> p u (g c)", u=2)
+                        .bitcast(BF16)
+                        .rearrange("p u (c e) -> p c u e", e=2),
+                        func=ACT.Square,
+                    )
+
+        def quantise(j, lo=0, hi=4096):
+            key = JOBS[j]
+            if key not in codes_of:
+                codes = q_pool.tile([P, 1024], U32, name="codes", tag="codes", align_bytes=64)
+                scales = q_pool.tile([P, 1024], U8, name="scales", tag="scales", align_bytes=64)
+                codes_of[key] = (codes, scales)
+            codes, scales = codes_of[key]
+            nc.vector.quantize_mx(
+                out=codes[:, lo // 4 : hi // 4].bitcast(FP8X4),
+                scales=scales[:, lo // 4 : hi // 4],
+                in_=grp[key][:, lo:hi],
+            )
+
         x_acc = {}
 
-        def x_out(h):
-            grp = grp_pool.tile([P, 4096], BF16, name="grp", tag="grp", align_bytes=64)
-            x_grp[h] = grp
-            dst = grp[:].bitcast(F32)
-            made = banks[("x", h)]
-            for b in range(3):
-                words_out(nc.scalar.copy, dst, made[b], b)
-            words_out(nc.vector.tensor_copy, dst, made[3], 3)
-
-        def x_quant(h):
-            x_q[h] = new_codes()
-            quantise(x_grp[h], x_q[h][0], x_q[h][1], 0, 4096)
-
         def x_matmuls(h):
-            codes, scales = x_q[h]
+            codes, scales = codes_of[("x", h)]
             made = []
-            for cc in range(2):
+            for c in range(2):
                 acc = acc_pool.tile([P, 4, OUT_F], F32, name="acc", tag="acc")
                 for t in range(4):
-                    col = 512 * cc + 128 * t
+                    cols = slice(512 * c + 128 * t, 512 * c + 128 * t + 128)
                     nc.tensor.matmul_mx(
                         out=acc[:, t, :],
-                        lhsT=codes[:, col : col + 128].bitcast(FP8X4),
-                        lhsT_scale=scales[:, col : col + 128],
+                        lhsT=codes[:, cols].bitcast(FP8X4),
+                        lhsT_scale=scales[:, cols],
                         rhs=w_codes[:].bitcast(FP8X4),
                         rhs_scale=w_scales[:],
                         start=True,
@@ -180,46 +206,18 @@ def tile_netgraphconvolution_t_kernel(tc, x, adj, weight, bias, out):
             x_acc[h] = made
 
         def sup_out(h):
-            nc.scalar.copy(
-                out=sup_grp[:, 2 * h, :, :], in_=x_acc[h][0][:].rearrange("p t w -> p w t")
-            )
-            nc.vector.tensor_copy(
-                out=sup_grp[:, 2 * h + 1, :, :], in_=x_acc[h][1][:].rearrange("p t w -> p w t")
-            )
-
-        a_grp = {}
-        a_q = {}
-
-        def a_out(i):
-            grp = grp_pool.tile([P, 4096], BF16, name="grp", tag="grp", align_bytes=64)
-            raw = raw_pool.tile([P, 2048], F32, name="raw", tag="raw")
-            a_grp[i] = (grp, raw)
-            made = banks[("a", i)]
-            for b in range(4):
-                if b < copies_of(i):
-                    words_out(nc.scalar.copy, raw, made[b], b)
-                else:
-                    nc.scalar.activation(
-                        out=grp[:, 1024 * b : 1024 * b + 1024].rearrange(
-                            "p (c u e) -> p c u e", u=2, e=2
-                        ),
-                        in_=made[b][:].bitcast(BF16).rearrange("p u (c e) -> p c u e", e=2),
-                        func=ACT.Square,
-                    )
-
-        def a_square(i):
-            grp, raw = a_grp[i]
-            raw_bf = raw[:].bitcast(BF16)
-            hi = 1024 * copies_of(i)
-            if hi > 0:
-                nc.vector.tensor_tensor(
-                    out=grp[:, 0:hi], in0=raw_bf[:, 0:hi], in1=raw_bf[:, 0:hi], op=ALU.mult
+            for c in range(2):
+                nc.scalar.copy(
+                    out=sup_grp[:, 2 * h + c, :, :],
+                    in_=x_acc[h][c][:].rearrange("p t w -> p w t"),
                 )
 
-        def a_quant(i, lo=0, hi=4096):
-            if lo == 0:
-                a_q[i] = new_codes()
-            quantise(a_grp[i][0], a_q[i][0], a_q[i][1], lo, hi)
+        def sup_quant(h):
+            nc.vector.quantize_mx(
+                out=sup_codes[:, 256 * h : 256 * h + 256].bitcast(FP8X4),
+                scales=sup_scales[:, 256 * h : 256 * h + 256],
+                in_=sup_grp[:].rearrange("p c w t -> p (c w t)")[:, 1024 * h : 1024 * h + 1024],
+            )
 
         units = [[4 * g, 4 * g + 1, 4 * g + 2, 4 * g + 3] for g in range(7)] + [[28, 29, 30], [31]]
         unit_of = {}
@@ -229,12 +227,12 @@ def tile_netgraphconvolution_t_kernel(tc, x, adj, weight, bias, out):
         unit_acc = {}
         unit_ep = {}
 
-        def a_matmuls(i, g_lo=0, g_hi=8):
+        def a_matmuls(i, g_lo=0, g_hi=8, first=0, final=7):
             n = unit_of[i]
-            if i == units[n][0] and g_lo == 0:
+            if i == units[n][0] and g_lo == first:
                 unit_acc[n] = acc_pool.tile([P, 4, OUT_F], F32, name="acc", tag="acc")
             acc = unit_acc[n]
-            codes, scales = a_q[i]
+            codes, scales = codes_of[("a", i)]
             s = i - units[n][0]
             for g in range(g_lo, g_hi):
                 cols = slice(128 * g, 128 * g + 128)
@@ -244,11 +242,9 @@ def tile_netgraphconvolution_t_kernel(tc, x, adj, weight, bias, out):
                     lhsT_scale=scales[:, cols],
                     rhs=sup_codes[:, cols].bitcast(FP8X4),
                     rhs_scale=sup_scales[:, cols],
-                    start=(g == 0),
-                    stop=(g == 7),
+                    start=(g == first),
+                    stop=(g == final),
                 )
-
-        bias_f = const.tile([P, OUT_F], F32, name="bias_f")
 
         def ep_first(n):
             k = len(units[n])
@@ -286,66 +282,81 @@ def tile_netgraphconvolution_t_kernel(tc, x, adj, weight, bias, out):
             s0 = first % 4
             nc.sync.dma_start(out=out_view[first // 4][:, s0 : s0 + k, :], in_=o[:, 0:k, :])
 
-        transposes(("x", 0))
-        for h in range(CHUNKS):
-            load_a(A_BUFS - CHUNKS + h)
-            if h + 1 < CHUNKS:
-                transposes(("x", h + 1))
+        last = len(JOBS) - 1
+        pre_square(0, 0, 2)
+        pre_square(0, 2, 4)
+        pre_square(0, 4, PRE)
+        transposes(0)
+        weight_out()
+        sup_ready = TILES + 4
+        waiting = []
+        post = {}
+        for j in range(last):
+            if j == 1:
+                evacuate(j, (2, 3))
+                evacuate(j, (0, 1), nc.vector.tensor_copy)
+                pre_square(2)
+                transposes(j + 1)
             else:
-                transposes(("a", 0))
-                load_a(A_BUFS)
-            x_out(h)
-            if h > 0:
-                sup_out(h - 1)
-            x_quant(h)
-            x_matmuls(h)
-        transposes(("a", 1))
-        load_a(A_BUFS + 1)
+                transposes(j + 1)
+                evacuate(j)
+            load(j + A_BUFS)
+            for name, n in post.get(j, []):
+                if name == "exp":
+                    ep_exp(n)
+                elif name == "sup":
+                    sup_out(n)
+            if j == 0:
+                weight_quant()
+            else:
+                quantise(j - 1)
+            if j > 0:
+                pre_square(j + 2)
+            for name, n in post.get(j, []):
+                if name == "supq":
+                    sup_quant(n)
+                    if n == 3:
+                        nc.vector.tensor_copy(out=bias_f[:], in_=bias_bf[:])
+                        sup_ready = j + 1
+                elif name == "first":
+                    ep_first(n)
+                elif name == "exp":
+                    ep_last(n)
+            if j >= 1:
+                kind, i = JOBS[j - 1]
+                if kind == "x":
+                    x_matmuls(i)
+                    post.setdefault(j + 1, []).append(("sup", i))
+                    post.setdefault(j + 2, []).append(("supq", i))
+                else:
+                    waiting.append(i)
+            if j >= sup_ready:
+                for i in waiting[:2]:
+                    a_matmuls(i)
+                    n = unit_of[i]
+                    if i == units[n][-1] and n < len(units) - 2:
+                        post.setdefault(j + 1, []).append(("first", n))
+                        post.setdefault(j + 2, []).append(("exp", n))
+                waiting = waiting[2:]
 
-        first_at = {}
-        exp_at = {}
-        last_at = {}
-        for n, rows in enumerate(units[:-2]):
-            first_at[rows[-1] + 2] = n
-            exp_at[rows[-1] + 3] = n
-            last_at[rows[-1] + 3] = n
-
-        for i in range(TILES - 1):
-            if i + 2 < TILES:
-                transposes(("a", i + 2))
-                load_a(i + 2 + A_BUFS)
-            a_out(i)
-            if i in exp_at:
-                ep_exp(exp_at[i])
-            a_square(i)
-            if i == 0:
-                sup_out(CHUNKS - 1)
-                nc.vector.quantize_mx(
-                    out=sup_codes[:].bitcast(FP8X4),
-                    scales=sup_scales[:],
-                    in_=sup_grp[:].rearrange("p c w t -> p (c w t)"),
-                )
-            if i == 3:
-                nc.vector.tensor_copy(out=bias_f[:], in_=bias_bf[:])
-            if i >= 1:
-                a_quant(i - 1)
-                a_matmuls(i - 1)
-            if i in first_at:
-                ep_first(first_at[i])
-            if i in last_at:
-                ep_last(last_at[i])
-
-        last = TILES - 1
-        a_out(last)
-        a_quant(last - 1)
-        a_matmuls(last - 1)
-        a_square(last)
+        evacuate(last, (2,))
+        quantise(last - 1)
+        evacuate(last, (3, 0, 1), nc.vector.tensor_copy)
+        for i in waiting:
+            a_matmuls(i)
+        a_matmuls(TILES - 2)
+        for j in (last, last + 1):
+            for name, n in post.get(j, []):
+                if name == "first":
+                    ep_first(n)
+                else:
+                    ep_exp(n)
+                    ep_last(n)
         ep_first(len(units) - 2)
         ep_exp(len(units) - 2)
-        cuts = END_CUTS
-        for c in range(len(cuts) - 1):
-            a_quant(last, cuts[c], cuts[c + 1])
-            a_matmuls(last, cuts[c] // 512, cuts[c + 1] // 512)
+        for c, (lo, hi) in enumerate(END_CUTS):
+            quantise(last, lo, hi)
+            a_matmuls(TILES - 1, lo // 512, hi // 512, END_CUTS[0][0] // 512, END_CUTS[-1][1] // 512 - 1)
             if c == 0:
                 ep_last(len(units) - 2)
         ep_first(len(units) - 1)

@@ -17,17 +17,20 @@ IN_F = 512
 OUT_F = 128
 TILES = NODES // P
 A_BUFS = 12
-PRE = 6
-PRE_COLS = 512 * PRE
-PRE_HALF = PRE_COLS // 4
-BANK_ORDER = (3, 0, 1, 2)
+X_TILES = 4
+LAG = 2
+X_PIECES = (4, 2, 1, 1)
+X_VECTOR_BANKS = (1, 3)
+END_VECTOR_BANKS = (2,)
 END_CUTS = ((3072, 4096), (0, 2048), (2048, 3072))
+BANK_ORDER = (3, 0, 1, 2)
 FLOPS = 2 * NODES * IN_F * OUT_F + 2 * NODES * NODES * OUT_F
 
-JOBS = (
-    [("a", 0), ("x", 0), ("a", 1), ("a", 2), ("x", 1), ("a", 3), ("a", 4), ("x", 2), ("a", 5), ("a", 6), ("x", 3)]
-    + [("a", i) for i in range(7, TILES)]
-)
+JOBS = [("x", h) for h in range(X_TILES)] + [("a", i) for i in range(TILES)]
+
+
+def pre_banks(i):
+    return 3 if i % 2 == 0 or i == TILES - 1 else 2
 
 
 def tile_netgraphconvolution_t_kernel(tc, x, adj, weight, bias, out):
@@ -35,15 +38,14 @@ def tile_netgraphconvolution_t_kernel(tc, x, adj, weight, bias, out):
     with ExitStack() as ctx:
         const = ctx.enter_context(tc.tile_pool(name="const", bufs=1))
         a_pool = ctx.enter_context(tc.tile_pool(name="a_pool", bufs=A_BUFS))
-        sq_pool = ctx.enter_context(tc.tile_pool(name="sq_pool", bufs=3))
-        grp_pool = ctx.enter_context(tc.tile_pool(name="grp_pool", bufs=3))
-        q_pool = ctx.enter_context(tc.tile_pool(name="q_pool", bufs=11))
+        grp_pool = ctx.enter_context(tc.tile_pool(name="grp_pool", bufs=4))
+        q_pool = ctx.enter_context(tc.tile_pool(name="q_pool", bufs=6))
         ep_pool = ctx.enter_context(tc.tile_pool(name="ep_pool", bufs=2))
         tp_pool = ctx.enter_context(tc.psum_pool(name="tp_pool", bufs=6))
         acc_pool = ctx.enter_context(tc.psum_pool(name="acc_pool", bufs=2))
         ctx.enter_context(tc.manual_schedule())
 
-        x_view = x.rearrange("(h p s) k -> h p (s k)", h=4, p=P, s=8)
+        x_view = x.rearrange("(n p s) k -> p n (s k)", n=8, p=P, s=4)
         w_view = weight.rearrange("(q t) c -> q (t c)", q=P, t=4)
         adj_view = adj.rearrange("(g p s) k -> g s p k", g=8, p=P, s=4)
         out_view = out.rearrange("(g p s) f -> g p s f", g=8, p=P, s=4)
@@ -57,69 +59,59 @@ def tile_netgraphconvolution_t_kernel(tc, x, adj, weight, bias, out):
 
         raw = {}
 
-        def load(j, order=(0,)):
+        def load(j):
             if j >= len(JOBS):
                 return
             kind, i = JOBS[j]
             t = a_pool.tile([P, 4096], BF16, name="a", tag="a")
-            src = x_view[i] if kind == "x" else adj_view[i // 4, i % 4]
-            width = 4096 // len(order)
-            for c in order:
-                cols = slice(width * c, width * c + width)
-                nc.sync.dma_start(out=t[:, cols], in_=src[:, cols])
             raw[JOBS[j]] = t
+            if kind == "a":
+                nc.sync.dma_start(out=t[:], in_=adj_view[i // 4, i % 4])
+            elif X_PIECES[i] == 1:
+                nc.sync.dma_start(
+                    out=t[:].rearrange("p (n k) -> p n k", n=2), in_=x_view[:, 2 * i : 2 * i + 2, :]
+                )
+            else:
+                width = 4096 // X_PIECES[i]
+                for lo in range(0, 4096, width):
+                    nc.sync.dma_start(
+                        out=t[:, lo : lo + width],
+                        in_=x_view[:, 2 * i + lo // 2048, lo % 2048 : lo % 2048 + width],
+                    )
 
-        squared = {}
-
-        def pre_square(j, lo=0, hi=PRE):
+        def pre_square(j):
             if j >= len(JOBS) or JOBS[j][0] == "x":
                 return
-            key = JOBS[j]
-            if lo == 0:
-                squared[key] = sq_pool.tile([P, PRE_COLS], BF16, name="sq", tag="sq")
-            src = raw[key][:, 512 * lo : 512 * hi].rearrange("p (q u v) -> p u q v", u=2, v=4)
-            dst = squared[key][:].rearrange("p (u q v) -> p u q v", u=2, v=4)[:, :, 64 * lo : 64 * hi, :]
-            nc.vector.tensor_tensor(out=dst, in0=src, in1=src, op=ALU.mult)
+            part = raw[JOBS[j]][:, 0 : 1024 * pre_banks(JOBS[j][1])]
+            nc.vector.tensor_tensor(out=part, in0=part, in1=part, op=ALU.mult)
 
         banks = {}
 
         def transposes(j):
             if j >= len(JOBS):
                 return
-            key = JOBS[j]
-            words = raw[key][:].bitcast(F32)
+            words = raw[JOBS[j]][:].bitcast(F32)
             made = {}
-            for b in range(4) if key[0] == "x" else BANK_ORDER:
-                tp = tp_pool.tile([P, 4, P], F32, name="tp", tag="tp")
-                if key[0] == "x":
-                    for v in range(2):
-                        s = 4 * (b // 2) + b % 2 + 2 * v if key[1] < PRE // 2 else b + 4 * v
-                        for e in range(2):
-                            nc.tensor.transpose(
-                                tp[:, 2 * v + e, :],
-                                words[:, 256 * s + e : 256 * s + 256 : 2],
-                                ident[:],
-                            )
-                else:
-                    for g in range(2):
-                        n = 2 * b + g
-                        for u in range(2):
-                            if n < PRE:
-                                lo = PRE_HALF * u + 128 * n
-                                src = squared[key][:].bitcast(F32)[:, lo : lo + 128]
-                            else:
-                                src = words[:, 256 * n + u : 256 * n + 256 : 2]
-                            nc.tensor.transpose(tp[:, 2 * u + g, :], src, ident[:])
+            for b in range(4) if JOBS[j][0] == "x" else BANK_ORDER:
+                tp = tp_pool.tile([P, 2, 256], F32, name="tp", tag="tp")
+                for g in range(2):
+                    for u in range(2):
+                        col = 512 * b + 256 * g
+                        nc.tensor.transpose(
+                            tp[:, u, 128 * g : 128 * g + 128],
+                            words[:, col + u : col + 256 : 2],
+                            ident[:],
+                        )
                 made[b] = tp
-            banks[key] = made
+            banks[JOBS[j]] = made
 
         w_raw = const.tile([P, 4, OUT_F], BF16, name="w_raw")
         bias_bf = const.tile([P, OUT_F], BF16, name="bias_bf")
         for j in range(A_BUFS):
-            load(j, ((3, 0, 1, 2), (0, 1), (1, 0))[j] if j < 3 else (0,))
-            if j == 1:
+            load(j)
+            if j == 0:
                 nc.sync.dma_start(out=w_raw[:].rearrange("p t c -> p (t c)"), in_=w_view)
-            if j == 7:
+            if j == 5:
                 nc.sync.dma_start(out=bias_bf[:], in_=bias.partition_broadcast(P))
 
         w_grp = const.tile([P, OUT_F, 4], BF16, name="w_grp", align_bytes=64)
@@ -143,31 +135,23 @@ def tile_netgraphconvolution_t_kernel(tc, x, adj, weight, bias, out):
         grp = {}
         codes_of = {}
 
-        def evacuate(j, skip=(), copy=nc.scalar.copy):
+        def evacuate(j, chosen, copy):
             key = JOBS[j]
             if key not in grp:
                 grp[key] = grp_pool.tile([P, 4096], BF16, name="grp", tag="grp", align_bytes=64)
             t = grp[key]
-            dst = t[:].bitcast(F32)
             for b, tp in banks[key].items():
-                if b in skip:
+                if b not in chosen:
                     continue
-                if key[0] == "x":
+                if key[0] == "x" or b < pre_banks(key[1]):
                     copy(
-                        out=dst.rearrange("p (c t q j) -> p t c q j", c=2, t=4, j=4)[:, b],
-                        in_=tp[:].rearrange("p j (c q) -> p c q j", c=2),
-                    )
-                elif 2 * b < PRE:
-                    copy(
-                        out=dst[:, 512 * b : 512 * b + 512].rearrange("p (c u) -> p c u", u=2),
-                        in_=tp[:].rearrange("p (u g) c -> p (g c) u", u=2),
+                        out=t[:].bitcast(F32)[:, 512 * b : 512 * b + 512].rearrange("p (c u) -> p c u", u=2),
+                        in_=tp[:].rearrange("p u c -> p c u"),
                     )
                 else:
                     nc.scalar.activation(
                         out=t[:, 1024 * b : 1024 * b + 1024].rearrange("p (c u e) -> p c u e", u=2, e=2),
-                        in_=tp[:].rearrange("p (u g) c -> p u (g c)", u=2)
-                        .bitcast(BF16)
-                        .rearrange("p u (c e) -> p c u e", e=2),
+                        in_=tp[:].bitcast(BF16).rearrange("p u (c e) -> p c u e", e=2),
                         func=ACT.Square,
                     )
 
@@ -212,11 +196,11 @@ def tile_netgraphconvolution_t_kernel(tc, x, adj, weight, bias, out):
                     in_=x_acc[h][c][:].rearrange("p t w -> p w t"),
                 )
 
-        def sup_quant(h):
+        def sup_quant():
             nc.vector.quantize_mx(
-                out=sup_codes[:, 256 * h : 256 * h + 256].bitcast(FP8X4),
-                scales=sup_scales[:, 256 * h : 256 * h + 256],
-                in_=sup_grp[:].rearrange("p c w t -> p (c w t)")[:, 1024 * h : 1024 * h + 1024],
+                out=sup_codes[:].bitcast(FP8X4),
+                scales=sup_scales[:],
+                in_=sup_grp[:].rearrange("p c w t -> p (c w t)"),
             )
 
         units = [[4 * g, 4 * g + 1, 4 * g + 2, 4 * g + 3] for g in range(7)] + [[28, 29, 30], [31]]
@@ -229,7 +213,7 @@ def tile_netgraphconvolution_t_kernel(tc, x, adj, weight, bias, out):
 
         def a_matmuls(i, g_lo=0, g_hi=8, first=0, final=7):
             n = unit_of[i]
-            if i == units[n][0] and g_lo == first:
+            if n not in unit_acc:
                 unit_acc[n] = acc_pool.tile([P, 4, OUT_F], F32, name="acc", tag="acc")
             acc = unit_acc[n]
             codes, scales = codes_of[("a", i)]
@@ -249,13 +233,18 @@ def tile_netgraphconvolution_t_kernel(tc, x, adj, weight, bias, out):
         def ep_first(n):
             k = len(units[n])
             v = ep_pool.tile([P, 4, OUT_F], F32, name="v", tag="v")
-            m = ep_pool.tile([P, 4, OUT_F], F32, name="m", tag="m")
             nc.vector.tensor_tensor(
                 out=v[:, 0:k, :],
                 in0=unit_acc[n][:, 0:k, :],
                 in1=bias_f[:].unsqueeze(1).to_broadcast([P, k, OUT_F]),
                 op=ALU.add,
             )
+            unit_ep[n] = (v, None)
+
+        def ep_min(n):
+            k = len(units[n])
+            v = unit_ep[n][0]
+            m = ep_pool.tile([P, 4, OUT_F], F32, name="m", tag="m")
             nc.vector.tensor_scalar_min(out=m[:, 0:k, :], in0=v[:, 0:k, :], scalar1=0.0)
             unit_ep[n] = (v, m)
 
@@ -283,82 +272,103 @@ def tile_netgraphconvolution_t_kernel(tc, x, adj, weight, bias, out):
             nc.sync.dma_start(out=out_view[first // 4][:, s0 : s0 + k, :], in_=o[:, 0:k, :])
 
         last = len(JOBS) - 1
-        pre_square(0, 0, 2)
-        pre_square(0, 2, 4)
-        pre_square(0, 4, PRE)
         transposes(0)
         weight_out()
-        sup_ready = TILES + 4
+        sup_ready = len(JOBS)
         waiting = []
-        post = {}
+        todo = {}
+
+        def plan(step, what, n):
+            todo.setdefault((step, what), []).append(n)
+
+        def due(step, what):
+            return todo.pop((step, what), [])
+
         for j in range(last):
-            if j == 1:
-                evacuate(j, (2, 3))
-                evacuate(j, (0, 1), nc.vector.tensor_copy)
-                pre_square(2)
-                transposes(j + 1)
+            if JOBS[j][0] == "x":
+                evacuate(j, [b for b in range(4) if b not in X_VECTOR_BANKS], nc.scalar.copy)
+                evacuate(j, X_VECTOR_BANKS, nc.vector.tensor_copy)
             else:
-                transposes(j + 1)
-                evacuate(j)
-            load(j + A_BUFS)
-            for name, n in post.get(j, []):
-                if name == "exp":
-                    ep_exp(n)
-                elif name == "sup":
-                    sup_out(n)
+                evacuate(j, range(4), nc.scalar.copy)
+            for n in due(j, "exp"):
+                ep_exp(n)
+            for n in due(j, "sup"):
+                sup_out(n)
+            for n in due(j, "last"):
+                ep_last(n)
             if j == 0:
                 weight_quant()
-            else:
-                quantise(j - 1)
-            if j > 0:
+            if j == X_TILES - 1:
+                pre_square(j + 1)
+            transposes(j + 1)
+            load(j + A_BUFS)
+            if j >= LAG:
+                quantise(j - LAG)
+            for n in due(j, "first"):
+                ep_first(n)
+                plan(j, "min", n)
+            if j >= X_TILES - 1:
                 pre_square(j + 2)
-            for name, n in post.get(j, []):
-                if name == "supq":
-                    sup_quant(n)
-                    if n == 3:
-                        nc.vector.tensor_copy(out=bias_f[:], in_=bias_bf[:])
-                        sup_ready = j + 1
-                elif name == "first":
-                    ep_first(n)
-                elif name == "exp":
-                    ep_last(n)
-            if j >= 1:
-                kind, i = JOBS[j - 1]
+            for n in due(j, "min"):
+                ep_min(n)
+            if due(j, "sup_quant"):
+                sup_quant()
+                nc.vector.tensor_copy(out=bias_f[:], in_=bias_bf[:])
+                sup_ready = j + 1
+            if j >= LAG:
+                kind, i = JOBS[j - LAG]
                 if kind == "x":
                     x_matmuls(i)
-                    post.setdefault(j + 1, []).append(("sup", i))
-                    post.setdefault(j + 2, []).append(("supq", i))
+                    plan(j + 1, "sup", i)
+                    if i == X_TILES - 1:
+                        plan(j + 2, "sup_quant", i)
                 else:
                     waiting.append(i)
             if j >= sup_ready:
                 for i in waiting[:2]:
                     a_matmuls(i)
                     n = unit_of[i]
-                    if i == units[n][-1] and n < len(units) - 2:
-                        post.setdefault(j + 1, []).append(("first", n))
-                        post.setdefault(j + 2, []).append(("exp", n))
+                    if i == units[n][-1]:
+                        plan(j + 1, "first", n)
+                        plan(j + 2, "exp", n)
+                        plan(j + 3, "last", n)
                 waiting = waiting[2:]
 
-        evacuate(last, (2,))
-        quantise(last - 1)
-        evacuate(last, (3, 0, 1), nc.vector.tensor_copy)
+        evacuate(last, [b for b in range(4) if b not in END_VECTOR_BANKS], nc.scalar.copy)
+        quantise(last - 2)
+        waiting.append(TILES - 3)
         for i in waiting:
             a_matmuls(i)
+        assert len(waiting) == 1
+        for n in due(last, "first"):
+            ep_first(n)
+            ep_min(n)
+        for n in due(last, "exp"):
+            ep_exp(n)
+        for n in due(last, "last"):
+            ep_last(n)
+        quantise(last - 1)
         a_matmuls(TILES - 2)
-        for j in (last, last + 1):
-            for name, n in post.get(j, []):
-                if name == "first":
-                    ep_first(n)
-                else:
-                    ep_exp(n)
+        evacuate(last, END_VECTOR_BANKS, nc.vector.tensor_copy)
+        for n in due(last + 1, "exp"):
+            ep_exp(n)
+        for what in ("last",):
+            for step in (last + 1, last + 2):
+                for n in due(step, what):
                     ep_last(n)
-        ep_first(len(units) - 2)
-        ep_exp(len(units) - 2)
+        n = len(units) - 2
         for c, (lo, hi) in enumerate(END_CUTS):
             quantise(last, lo, hi)
             a_matmuls(TILES - 1, lo // 512, hi // 512, END_CUTS[0][0] // 512, END_CUTS[-1][1] // 512 - 1)
             if c == 0:
-                ep_last(len(units) - 2)
-        ep_first(len(units) - 1)
-        ep_exp(len(units) - 1)
-        ep_last(len(units) - 1)
+                ep_first(n)
+            elif c == 1:
+                ep_min(n)
+                ep_exp(n)
+        n += 1
+        ep_first(n)
+        ep_last(n - 1)
+        ep_min(n)
+        ep_exp(n)
+        ep_last(n)
+        assert not todo

@@ -19,18 +19,25 @@ TILES = NODES // P
 A_BUFS = 12
 X_TILES = 4
 LAG = 2
-X_PIECES = (4, 2, 1, 1)
+A0_CUTS = (3072, 2048, 1024, 0)
 X_VECTOR_BANKS = (1, 3)
-END_VECTOR_BANKS = (2,)
-END_CUTS = ((3072, 4096), (0, 2048), (2048, 3072))
-BANK_ORDER = (3, 0, 1, 2)
+END_VECTOR_BANKS = (0,)
+END_CUTS = ((2048, 4096), (0, 1024), (1024, 2048))
+BANK_ORDER = (3, 2, 1, 0)
 FLOPS = 2 * NODES * IN_F * OUT_F + 2 * NODES * NODES * OUT_F
 
-JOBS = [("x", h) for h in range(X_TILES)] + [("a", i) for i in range(TILES)]
+JOBS = [("a", 0), ("a", 1), ("a", 2), ("x", 0), ("x", 1), ("a", 3), ("x", 2), ("x", 3)] + [
+    ("a", i) for i in range(4, TILES)
+]
+LATE = (5,)
 
 
 def pre_banks(i):
-    return 3 if i % 2 == 0 or i == TILES - 1 else 2
+    if i >= TILES - 2:
+        return 1
+    if i < TILES - 8:
+        return 2 if i % 4 == 3 else 3
+    return 3 if i % 2 == 0 else 2
 
 
 def tile_netgraphconvolution_t_kernel(tc, x, adj, weight, bias, out):
@@ -39,7 +46,7 @@ def tile_netgraphconvolution_t_kernel(tc, x, adj, weight, bias, out):
         const = ctx.enter_context(tc.tile_pool(name="const", bufs=1))
         a_pool = ctx.enter_context(tc.tile_pool(name="a_pool", bufs=A_BUFS))
         grp_pool = ctx.enter_context(tc.tile_pool(name="grp_pool", bufs=4))
-        q_pool = ctx.enter_context(tc.tile_pool(name="q_pool", bufs=6))
+        q_pool = ctx.enter_context(tc.tile_pool(name="q_pool", bufs=10))
         ep_pool = ctx.enter_context(tc.tile_pool(name="ep_pool", bufs=2))
         tp_pool = ctx.enter_context(tc.psum_pool(name="tp_pool", bufs=6))
         acc_pool = ctx.enter_context(tc.psum_pool(name="acc_pool", bufs=2))
@@ -65,24 +72,19 @@ def tile_netgraphconvolution_t_kernel(tc, x, adj, weight, bias, out):
             kind, i = JOBS[j]
             t = a_pool.tile([P, 4096], BF16, name="a", tag="a")
             raw[JOBS[j]] = t
-            if kind == "a":
+            if j == 0:
+                for lo in A0_CUTS:
+                    nc.sync.dma_start(out=t[:, lo : lo + 1024], in_=adj_view[0, 0][:, lo : lo + 1024])
+            elif kind == "a":
                 nc.sync.dma_start(out=t[:], in_=adj_view[i // 4, i % 4])
-            elif X_PIECES[i] == 1:
-                nc.sync.dma_start(
-                    out=t[:].rearrange("p (n k) -> p n k", n=2), in_=x_view[:, 2 * i : 2 * i + 2, :]
-                )
             else:
-                width = 4096 // X_PIECES[i]
-                for lo in range(0, 4096, width):
-                    nc.sync.dma_start(
-                        out=t[:, lo : lo + width],
-                        in_=x_view[:, 2 * i + lo // 2048, lo % 2048 : lo % 2048 + width],
-                    )
+                for n in range(2):
+                    nc.sync.dma_start(out=t[:, 2048 * n : 2048 * n + 2048], in_=x_view[:, 2 * i + n, :])
 
-        def pre_square(j):
+        def pre_square(j, lo=0, hi=4096):
             if j >= len(JOBS) or JOBS[j][0] == "x":
                 return
-            part = raw[JOBS[j]][:, 0 : 1024 * pre_banks(JOBS[j][1])]
+            part = raw[JOBS[j]][:, lo : min(hi, 1024 * pre_banks(JOBS[j][1]))]
             nc.vector.tensor_tensor(out=part, in0=part, in1=part, op=ALU.mult)
 
         banks = {}
@@ -111,7 +113,7 @@ def tile_netgraphconvolution_t_kernel(tc, x, adj, weight, bias, out):
             load(j)
             if j == 0:
                 nc.sync.dma_start(out=w_raw[:].rearrange("p t c -> p (t c)"), in_=w_view)
-            if j == 5:
+            if j == 8:
                 nc.sync.dma_start(out=bias_bf[:], in_=bias.partition_broadcast(P))
 
         w_grp = const.tile([P, OUT_F, 4], BF16, name="w_grp", align_bytes=64)
@@ -272,6 +274,8 @@ def tile_netgraphconvolution_t_kernel(tc, x, adj, weight, bias, out):
             nc.sync.dma_start(out=out_view[first // 4][:, s0 : s0 + k, :], in_=o[:, 0:k, :])
 
         last = len(JOBS) - 1
+        for lo in A0_CUTS[1:]:
+            pre_square(0, lo, lo + 1024)
         transposes(0)
         weight_out()
         sup_ready = len(JOBS)
@@ -298,7 +302,7 @@ def tile_netgraphconvolution_t_kernel(tc, x, adj, weight, bias, out):
                 ep_last(n)
             if j == 0:
                 weight_quant()
-            if j == X_TILES - 1:
+            if j == 0 or j + 1 in LATE:
                 pre_square(j + 1)
             transposes(j + 1)
             load(j + A_BUFS)
@@ -307,7 +311,7 @@ def tile_netgraphconvolution_t_kernel(tc, x, adj, weight, bias, out):
             for n in due(j, "first"):
                 ep_first(n)
                 plan(j, "min", n)
-            if j >= X_TILES - 1:
+            if j + 2 not in LATE:
                 pre_square(j + 2)
             for n in due(j, "min"):
                 ep_min(n)
@@ -334,41 +338,29 @@ def tile_netgraphconvolution_t_kernel(tc, x, adj, weight, bias, out):
                         plan(j + 3, "last", n)
                 waiting = waiting[2:]
 
+        for n in due(last, "exp"):
+            ep_exp(n)
         evacuate(last, [b for b in range(4) if b not in END_VECTOR_BANKS], nc.scalar.copy)
         quantise(last - 2)
         waiting.append(TILES - 3)
         for i in waiting:
             a_matmuls(i)
-        assert len(waiting) == 1
-        for n in due(last, "first"):
-            ep_first(n)
-            ep_min(n)
-        for n in due(last, "exp"):
-            ep_exp(n)
-        for n in due(last, "last"):
-            ep_last(n)
         quantise(last - 1)
         a_matmuls(TILES - 2)
         evacuate(last, END_VECTOR_BANKS, nc.vector.tensor_copy)
-        for n in due(last + 1, "exp"):
-            ep_exp(n)
-        for what in ("last",):
-            for step in (last + 1, last + 2):
-                for n in due(step, what):
-                    ep_last(n)
-        n = len(units) - 2
+        for n in due(last + 1, "last"):
+            ep_last(n)
+        n = len(units) - 1
         for c, (lo, hi) in enumerate(END_CUTS):
             quantise(last, lo, hi)
             a_matmuls(TILES - 1, lo // 512, hi // 512, END_CUTS[0][0] // 512, END_CUTS[-1][1] // 512 - 1)
             if c == 0:
-                ep_first(n)
-            elif c == 1:
-                ep_min(n)
-                ep_exp(n)
-        n += 1
+                ep_first(n - 1)
+        ep_min(n - 1)
+        ep_exp(n - 1)
         ep_first(n)
-        ep_last(n - 1)
         ep_min(n)
         ep_exp(n)
+        ep_last(n - 1)
         ep_last(n)
-        assert not todo
+        assert not todo and len(waiting) == 1

@@ -46,7 +46,7 @@ def tile_netgraphconvolution_t_kernel(tc, x, adj, weight, bias, out):
         const = ctx.enter_context(tc.tile_pool(name="const", bufs=1))
         a_pool = ctx.enter_context(tc.tile_pool(name="a_pool", bufs=A_BUFS))
         grp_pool = ctx.enter_context(tc.tile_pool(name="grp_pool", bufs=4))
-        q_pool = ctx.enter_context(tc.tile_pool(name="q_pool", bufs=10))
+        q_pool = ctx.enter_context(tc.tile_pool(name="q_pool", bufs=11))
         ep_pool = ctx.enter_context(tc.tile_pool(name="ep_pool", bufs=2))
         tp_pool = ctx.enter_context(tc.psum_pool(name="tp_pool", bufs=6))
         acc_pool = ctx.enter_context(tc.psum_pool(name="acc_pool", bufs=2))
@@ -279,7 +279,7 @@ def tile_netgraphconvolution_t_kernel(tc, x, adj, weight, bias, out):
         transposes(0)
         weight_out()
         sup_ready = len(JOBS)
-        waiting = []
+        ready = []
         todo = {}
 
         def plan(step, what, n):
@@ -289,6 +289,24 @@ def tile_netgraphconvolution_t_kernel(tc, x, adj, weight, bias, out):
             return todo.pop((step, what), [])
 
         for j in range(last):
+            for i in ready:
+                if JOBS[i][0] == "x":
+                    h = JOBS[i][1]
+                    x_matmuls(h)
+                    plan(j, "sup", h)
+                    if h == X_TILES - 1:
+                        plan(j + 1, "sup_quant", h)
+            ready = [i for i in ready if JOBS[i][0] == "a"]
+            if j >= sup_ready:
+                for i in ready[:2]:
+                    r = JOBS[i][1]
+                    a_matmuls(r)
+                    n = unit_of[r]
+                    if r == units[n][-1]:
+                        plan(j, "first", n)
+                        plan(j + 1, "exp", n)
+                        plan(j + 2, "last", n)
+                ready = ready[2:]
             if JOBS[j][0] == "x":
                 evacuate(j, [b for b in range(4) if b not in X_VECTOR_BANKS], nc.scalar.copy)
                 evacuate(j, X_VECTOR_BANKS, nc.vector.tensor_copy)
@@ -320,36 +338,21 @@ def tile_netgraphconvolution_t_kernel(tc, x, adj, weight, bias, out):
                 nc.vector.tensor_copy(out=bias_f[:], in_=bias_bf[:])
                 sup_ready = j + 1
             if j >= LAG:
-                kind, i = JOBS[j - LAG]
-                if kind == "x":
-                    x_matmuls(i)
-                    plan(j + 1, "sup", i)
-                    if i == X_TILES - 1:
-                        plan(j + 2, "sup_quant", i)
-                else:
-                    waiting.append(i)
-            if j >= sup_ready:
-                for i in waiting[:2]:
-                    a_matmuls(i)
-                    n = unit_of[i]
-                    if i == units[n][-1]:
-                        plan(j + 1, "first", n)
-                        plan(j + 2, "exp", n)
-                        plan(j + 3, "last", n)
-                waiting = waiting[2:]
+                ready.append(j - LAG)
 
         for n in due(last, "exp"):
             ep_exp(n)
         evacuate(last, [b for b in range(4) if b not in END_VECTOR_BANKS], nc.scalar.copy)
+        for i in ready:
+            a_matmuls(JOBS[i][1])
         quantise(last - 2)
-        waiting.append(TILES - 3)
-        for i in waiting:
-            a_matmuls(i)
+        a_matmuls(TILES - 3)
         quantise(last - 1)
         a_matmuls(TILES - 2)
         evacuate(last, END_VECTOR_BANKS, nc.vector.tensor_copy)
-        for n in due(last + 1, "last"):
-            ep_last(n)
+        for step in (last, last + 1):
+            for n in due(step, "last"):
+                ep_last(n)
         n = len(units) - 1
         for c, (lo, hi) in enumerate(END_CUTS):
             quantise(last, lo, hi)
@@ -363,4 +366,4 @@ def tile_netgraphconvolution_t_kernel(tc, x, adj, weight, bias, out):
         ep_exp(n)
         ep_last(n - 1)
         ep_last(n)
-        assert not todo and len(waiting) == 1
+        assert not todo and len(ready) == 1

@@ -19,11 +19,12 @@ TILES = NODES // P
 A_BUFS = 12
 X_TILES = 4
 LAG = 2
-A0_CUTS = (3072, 2048, 1024, 0)
+A0_CUTS = (3072, 0, 1024, 2048)
 X_VECTOR_BANKS = (1, 3)
 END_VECTOR_BANKS = (0,)
-END_CUTS = ((2048, 4096), (0, 1024), (1024, 2048))
-BANK_ORDER = (3, 2, 1, 0)
+END_CUTS = ((3072, 4096), (0, 2048), (2048, 3072))
+MIXED = 2
+BANK_ORDER = (3, 0, 1, 2)
 FLOPS = 2 * NODES * IN_F * OUT_F + 2 * NODES * NODES * OUT_F
 
 JOBS = [("a", 0), ("a", 1), ("a", 2), ("x", 0), ("x", 1), ("a", 3), ("x", 2), ("x", 3)] + [
@@ -33,11 +34,7 @@ LATE = (5,)
 
 
 def pre_banks(i):
-    if i >= TILES - 2:
-        return 1
-    if i < TILES - 8:
-        return 2 if i % 4 == 3 else 3
-    return 3 if i % 2 == 0 else 2
+    return 3 if i % 2 == 0 and i < TILES - 2 else 2
 
 
 def tile_netgraphconvolution_t_kernel(tc, x, adj, weight, bias, out):
@@ -45,8 +42,9 @@ def tile_netgraphconvolution_t_kernel(tc, x, adj, weight, bias, out):
     with ExitStack() as ctx:
         const = ctx.enter_context(tc.tile_pool(name="const", bufs=1))
         a_pool = ctx.enter_context(tc.tile_pool(name="a_pool", bufs=A_BUFS))
+        sq_pool = ctx.enter_context(tc.tile_pool(name="sq_pool", bufs=3))
         grp_pool = ctx.enter_context(tc.tile_pool(name="grp_pool", bufs=4))
-        q_pool = ctx.enter_context(tc.tile_pool(name="q_pool", bufs=11))
+        q_pool = ctx.enter_context(tc.tile_pool(name="q_pool", bufs=10))
         ep_pool = ctx.enter_context(tc.tile_pool(name="ep_pool", bufs=2))
         tp_pool = ctx.enter_context(tc.psum_pool(name="tp_pool", bufs=6))
         acc_pool = ctx.enter_context(tc.psum_pool(name="acc_pool", bufs=2))
@@ -59,10 +57,18 @@ def tile_netgraphconvolution_t_kernel(tc, x, adj, weight, bias, out):
 
         ident = const.tile([P, P], F32, name="ident")
         make_identity(nc, ident[:])
+        perm = const.tile([P, P], F32, name="perm")
+        nc.vector.tensor_copy(
+            out=perm[:].rearrange("p (u m v) -> p u m v", u=2, m=16),
+            in_=ident[:].rearrange("p (m u v) -> p u m v", u=2, m=16),
+        )
 
         warm = const.tile([P, 2], F32, name="warm")
         nc.vector.memset(warm[:, 0:1], 0.0)
         nc.scalar.activation(out=warm[:, 1:2], in_=warm[:, 0:1], func=ACT.Exp)
+
+        def mixed_x(key):
+            return key[0] == "x" and key[1] < MIXED
 
         raw = {}
 
@@ -81,31 +87,50 @@ def tile_netgraphconvolution_t_kernel(tc, x, adj, weight, bias, out):
                 for n in range(2):
                     nc.sync.dma_start(out=t[:, 2048 * n : 2048 * n + 2048], in_=x_view[:, 2 * i + n, :])
 
-        def pre_square(j, lo=0, hi=4096):
+        squared = {}
+
+        def pre_square(j, chosen=(0, 1, 2)):
             if j >= len(JOBS) or JOBS[j][0] == "x":
                 return
-            part = raw[JOBS[j]][:, lo : min(hi, 1024 * pre_banks(JOBS[j][1]))]
-            nc.vector.tensor_tensor(out=part, in0=part, in1=part, op=ALU.mult)
+            key = JOBS[j]
+            if key not in squared:
+                squared[key] = sq_pool.tile([P, 1024 * MIXED], BF16, name="sq", tag="sq")
+            mixed = [b for b in chosen if b < MIXED]
+            if mixed:
+                lo, hi = mixed[0], mixed[-1] + 1
+                src = raw[key][:, 1024 * lo : 1024 * hi].rearrange("p (q u v) -> p u q v", u=2, v=16)
+                dst = squared[key][:].rearrange("p (u q v) -> p u q v", u=2, v=16)
+                nc.vector.tensor_tensor(out=dst[:, :, 32 * lo : 32 * hi, :], in0=src, in1=src, op=ALU.mult)
+            for b in chosen:
+                if MIXED <= b < pre_banks(key[1]):
+                    part = raw[key][:, 1024 * b : 1024 * b + 1024]
+                    nc.vector.tensor_tensor(out=part, in0=part, in1=part, op=ALU.mult)
 
         banks = {}
 
         def transposes(j):
             if j >= len(JOBS):
                 return
-            words = raw[JOBS[j]][:].bitcast(F32)
+            key = JOBS[j]
+            words = raw[key][:].bitcast(F32)
             made = {}
-            for b in range(4) if JOBS[j][0] == "x" else BANK_ORDER:
-                tp = tp_pool.tile([P, 2, 256], F32, name="tp", tag="tp")
+            for b in range(4) if key[0] == "x" else BANK_ORDER:
+                tp = tp_pool.tile([P, 4, P], F32, name="tp", tag="tp")
                 for g in range(2):
                     for u in range(2):
                         col = 512 * b + 256 * g
-                        nc.tensor.transpose(
-                            tp[:, u, 128 * g : 128 * g + 128],
-                            words[:, col + u : col + 256 : 2],
-                            ident[:],
-                        )
+                        if mixed_x(key):
+                            col = 1024 * (b // 2) + 256 * (2 * g + b % 2)
+                            region, src, order = 2 * g + u, words[:, col + u : col + 256 : 2], perm
+                        elif key[0] == "a" and b < MIXED:
+                            col = 512 * u + 128 * (2 * b + g)
+                            region, order = 2 * u + g, ident
+                            src = squared[key][:].bitcast(F32)[:, col : col + 128]
+                        else:
+                            region, src, order = 2 * u + g, words[:, col + u : col + 256 : 2], ident
+                        nc.tensor.transpose(tp[:, region, :], src, order[:])
                 made[b] = tp
-            banks[JOBS[j]] = made
+            banks[key] = made
 
         w_raw = const.tile([P, 4, OUT_F], BF16, name="w_raw")
         bias_bf = const.tile([P, OUT_F], BF16, name="bias_bf")
@@ -145,15 +170,22 @@ def tile_netgraphconvolution_t_kernel(tc, x, adj, weight, bias, out):
             for b, tp in banks[key].items():
                 if b not in chosen:
                     continue
-                if key[0] == "x" or b < pre_banks(key[1]):
+                halves = tp[:].rearrange("p (u g) c -> p u (g c)", u=2)
+                if mixed_x(key):
+                    dst = t[:].bitcast(F32).rearrange("p (n u e q j) -> p n e u q j", n=2, u=2, e=2, j=4)
+                    copy(
+                        out=dst[:, b // 2, b % 2],
+                        in_=tp[:].rearrange("p j (u q) -> p u q j", u=2),
+                    )
+                elif key[0] == "x" or b < pre_banks(key[1]):
                     copy(
                         out=t[:].bitcast(F32)[:, 512 * b : 512 * b + 512].rearrange("p (c u) -> p c u", u=2),
-                        in_=tp[:].rearrange("p u c -> p c u"),
+                        in_=halves.rearrange("p u c -> p c u"),
                     )
                 else:
                     nc.scalar.activation(
                         out=t[:, 1024 * b : 1024 * b + 1024].rearrange("p (c u e) -> p c u e", u=2, e=2),
-                        in_=tp[:].bitcast(BF16).rearrange("p u (c e) -> p c u e", e=2),
+                        in_=halves.bitcast(BF16).rearrange("p u (c e) -> p c u e", e=2),
                         func=ACT.Square,
                     )
 
@@ -275,7 +307,7 @@ def tile_netgraphconvolution_t_kernel(tc, x, adj, weight, bias, out):
 
         last = len(JOBS) - 1
         for lo in A0_CUTS[1:]:
-            pre_square(0, lo, lo + 1024)
+            pre_square(0, (lo // 1024,))
         transposes(0)
         weight_out()
         sup_ready = len(JOBS)
@@ -336,7 +368,7 @@ def tile_netgraphconvolution_t_kernel(tc, x, adj, weight, bias, out):
             if due(j, "sup_quant"):
                 sup_quant()
                 nc.vector.tensor_copy(out=bias_f[:], in_=bias_bf[:])
-                sup_ready = j + 1
+                sup_ready = j + 2
             if j >= LAG:
                 ready.append(j - LAG)
 

@@ -34,7 +34,7 @@ LATE = (5,)
 
 
 def pre_banks(i):
-    return 3 if i % 2 == 0 and i < TILES - 2 else 2
+    return 3 if (i % 5 % 2 == 0) and i < TILES - 2 else 2
 
 
 def tile_netgraphconvolution_t_kernel(tc, x, adj, weight, bias, out):
@@ -94,17 +94,19 @@ def tile_netgraphconvolution_t_kernel(tc, x, adj, weight, bias, out):
                 return
             key = JOBS[j]
             if key not in squared:
-                squared[key] = sq_pool.tile([P, 1024 * MIXED], BF16, name="sq", tag="sq")
+                squared[key] = sq_pool.tile([P, 3072], BF16, name="sq", tag="sq")
             mixed = [b for b in chosen if b < MIXED]
             if mixed:
                 lo, hi = mixed[0], mixed[-1] + 1
                 src = raw[key][:, 1024 * lo : 1024 * hi].rearrange("p (q u v) -> p u q v", u=2, v=16)
-                dst = squared[key][:].rearrange("p (u q v) -> p u q v", u=2, v=16)
+                dst = squared[key][:, 0 : 1024 * MIXED].rearrange("p (u q v) -> p u q v", u=2, v=16)
                 nc.vector.tensor_tensor(out=dst[:, :, 32 * lo : 32 * hi, :], in0=src, in1=src, op=ALU.mult)
             for b in chosen:
                 if MIXED <= b < pre_banks(key[1]):
                     part = raw[key][:, 1024 * b : 1024 * b + 1024]
-                    nc.vector.tensor_tensor(out=part, in0=part, in1=part, op=ALU.mult)
+                    nc.vector.tensor_tensor(
+                        out=squared[key][:, 1024 * b : 1024 * b + 1024], in0=part, in1=part, op=ALU.mult
+                    )
 
         banks = {}
 
@@ -127,7 +129,11 @@ def tile_netgraphconvolution_t_kernel(tc, x, adj, weight, bias, out):
                             region, order = 2 * u + g, ident
                             src = squared[key][:].bitcast(F32)[:, col : col + 128]
                         else:
-                            region, src, order = 2 * u + g, words[:, col + u : col + 256 : 2], ident
+                            region, order = 2 * u + g, ident
+                            whole = words
+                            if key[0] == "a" and b < pre_banks(key[1]):
+                                whole = squared[key][:].bitcast(F32)
+                            src = whole[:, col + u : col + 256 : 2]
                         nc.tensor.transpose(tp[:, region, :], src, order[:])
                 made[b] = tp
             banks[key] = made

@@ -18,23 +18,21 @@ OUT_F = 128
 TILES = NODES // P
 A_BUFS = 12
 X_TILES = 4
-LAG = 2
+LAG = 1
 A0_CUTS = (3072, 0, 1024, 2048)
-X_VECTOR_BANKS = (1, 3)
+X_VECTOR_BANKS = (3,)
 END_VECTOR_BANKS = (0,)
 END_CUTS = ((3072, 4096), (0, 2048), (2048, 3072))
 MIXED = 2
 BANK_ORDER = (3, 0, 1, 2)
 FLOPS = 2 * NODES * IN_F * OUT_F + 2 * NODES * NODES * OUT_F
 
-JOBS = [("a", 0), ("a", 1), ("a", 2), ("x", 0), ("x", 1), ("a", 3), ("x", 2), ("x", 3)] + [
-    ("a", i) for i in range(4, TILES)
-]
-LATE = (5,)
+JOBS = [("a", i) for i in range(4)] + [("x", h) for h in range(X_TILES)] + [("a", i) for i in range(4, TILES)]
+LATE = (3,)
 
 
 def pre_banks(i):
-    return 3 if (i % 5 % 2 == 0) and i < TILES - 2 else 2
+    return 3 if (i % 3 < 2) and i < TILES - 2 else 2
 
 
 def tile_netgraphconvolution_t_kernel(tc, x, adj, weight, bias, out):
@@ -142,7 +140,7 @@ def tile_netgraphconvolution_t_kernel(tc, x, adj, weight, bias, out):
         bias_bf = const.tile([P, OUT_F], BF16, name="bias_bf")
         for j in range(A_BUFS):
             load(j)
-            if j == 0:
+            if j == 2:
                 nc.sync.dma_start(out=w_raw[:].rearrange("p t c -> p (t c)"), in_=w_view)
             if j == 8:
                 nc.sync.dma_start(out=bias_bf[:], in_=bias.partition_broadcast(P))
@@ -315,7 +313,6 @@ def tile_netgraphconvolution_t_kernel(tc, x, adj, weight, bias, out):
         for lo in A0_CUTS[1:]:
             pre_square(0, (lo // 1024,))
         transposes(0)
-        weight_out()
         sup_ready = len(JOBS)
         ready = []
         todo = {}
@@ -356,7 +353,9 @@ def tile_netgraphconvolution_t_kernel(tc, x, adj, weight, bias, out):
                 sup_out(n)
             for n in due(j, "last"):
                 ep_last(n)
-            if j == 0:
+            if j == 2:
+                weight_out()
+            if j == 3:
                 weight_quant()
             if j == 0 or j + 1 in LATE:
                 pre_square(j + 1)
@@ -383,8 +382,6 @@ def tile_netgraphconvolution_t_kernel(tc, x, adj, weight, bias, out):
         evacuate(last, [b for b in range(4) if b not in END_VECTOR_BANKS], nc.scalar.copy)
         for i in ready:
             a_matmuls(JOBS[i][1])
-        quantise(last - 2)
-        a_matmuls(TILES - 3)
         quantise(last - 1)
         a_matmuls(TILES - 2)
         evacuate(last, END_VECTOR_BANKS, nc.vector.tensor_copy)

@@ -332,8 +332,8 @@ def tile_netgraphconvolution_t_kernel(tc, x, adj, weight, bias, out):
                     if h == X_TILES - 1:
                         plan(j + 1, "sup_quant", h)
             ready = [i for i in ready if JOBS[i][0] == "a"]
-            if j >= sup_ready:
-                for i in ready[:2]:
+            if j >= sup_ready and j % 2 == 0:
+                for i in ready[:4]:
                     r = JOBS[i][1]
                     a_matmuls(r)
                     n = unit_of[r]
@@ -341,7 +341,7 @@ def tile_netgraphconvolution_t_kernel(tc, x, adj, weight, bias, out):
                         plan(j, "first", n)
                         plan(j + 1, "exp", n)
                         plan(j + 2, "last", n)
-                ready = ready[2:]
+                ready = ready[4:]
             if JOBS[j][0] == "x":
                 evacuate(j, [b for b in range(4) if b not in X_VECTOR_BANKS], nc.scalar.copy)
                 evacuate(j, X_VECTOR_BANKS, nc.vector.tensor_copy)

from contextlib import ExitStack

import concourse.mybir as mybir
from concourse.masks import make_identity

F32 = mybir.dt.float32
BF16 = mybir.dt.bfloat16
U32 = mybir.dt.uint32
U8 = mybir.dt.uint8
FP8X4 = mybir.dt.float8_e4m3fn_x4
ACT = mybir.ActivationFunctionType
ALU = mybir.AluOpType

P = 128
NODES = 4096
IN_F = 512
OUT_F = 128
TILES = NODES // P
A_BUFS = 12
X_TILES = 4
LAG = 1
A0_CUTS = (3072, 0, 1024, 2048)
X_VECTOR_BANKS = (3,)
END_VECTOR_BANKS = (0,)
END_CUTS = ((3072, 4096), (0, 2048), (2048, 3072))
MIXED = 2
BANK_ORDER = (3, 0, 1, 2)
FLOPS = 2 * NODES * IN_F * OUT_F + 2 * NODES * NODES * OUT_F

JOBS = [("a", i) for i in range(4)] + [("x", h) for h in range(X_TILES)] + [("a", i) for i in range(4, TILES)]
LATE = (3,)


def pre_banks(i):
    return 3 if (i % 3 < 2) and i < TILES - 2 else 2


def tile_netgraphconvolution_t_kernel(tc, x, adj, weight, bias, out):
    nc = tc.nc
    with ExitStack() as ctx:
        const = ctx.enter_context(tc.tile_pool(name="const", bufs=1))
        a_pool = ctx.enter_context(tc.tile_pool(name="a_pool", bufs=A_BUFS))
        sq_pool = ctx.enter_context(tc.tile_pool(name="sq_pool", bufs=3))
        grp_pool = ctx.enter_context(tc.tile_pool(name="grp_pool", bufs=4))
        q_pool = ctx.enter_context(tc.tile_pool(name="q_pool", bufs=10))
        ep_pool = ctx.enter_context(tc.tile_pool(name="ep_pool", bufs=2))
        tp_pool = ctx.enter_context(tc.psum_pool(name="tp_pool", bufs=6))
        acc_pool = ctx.enter_context(tc.psum_pool(name="acc_pool", bufs=2))
        ctx.enter_context(tc.manual_schedule())

        x_view = x.rearrange("(n p s) k -> p n (s k)", n=8, p=P, s=4)
        w_view = weight.rearrange("(q t) c -> q (t c)", q=P, t=4)
        adj_view = adj.rearrange("(g p s) k -> g s p k", g=8, p=P, s=4)
        out_view = out.rearrange("(g p s) f -> g p s f", g=8, p=P, s=4)

        ident = const.tile([P, P], F32, name="ident")
        make_identity(nc, ident[:])
        perm = const.tile([P, P], F32, name="perm")
        nc.vector.tensor_copy(
            out=perm[:].rearrange("p (u m v) -> p u m v", u=2, m=16),
            in_=ident[:].rearrange("p (m u v) -> p u m v", u=2, m=16),
        )

        warm = const.tile([P, 2], F32, name="warm")
        nc.vector.memset(warm[:, 0:1], 0.0)
        nc.scalar.activation(out=warm[:, 1:2], in_=warm[:, 0:1], func=ACT.Exp)

        def mixed_x(key):
            return key[0] == "x" and key[1] < MIXED

        raw = {}

        def load(j):
            if j >= len(JOBS):
                return
            kind, i = JOBS[j]
            t = a_pool.tile([P, 4096], BF16, name="a", tag="a")
            raw[JOBS[j]] = t
            if j == 0:
                for lo in A0_CUTS:
                    nc.sync.dma_start(out=t[:, lo : lo + 1024], in_=adj_view[0, 0][:, lo : lo + 1024])
            elif kind == "a":
                nc.sync.dma_start(out=t[:], in_=adj_view[i // 4, i % 4])
            else:
                for n in range(2):
                    nc.sync.dma_start(out=t[:, 2048 * n : 2048 * n + 2048], in_=x_view[:, 2 * i + n, :])

        squared = {}

        def pre_square(j, chosen=(0, 1, 2)):
            if j >= len(JOBS) or JOBS[j][0] == "x":
                return
            key = JOBS[j]
            if key not in squared:
                squared[key] = sq_pool.tile([P, 3072], BF16, name="sq", tag="sq")
            mixed = [b for b in chosen if b < MIXED]
            if mixed:
                lo, hi = mixed[0], mixed[-1] + 1
                src = raw[key][:, 1024 * lo : 1024 * hi].rearrange("p (q u v) -> p u q v", u=2, v=16)
                dst = squared[key][:, 0 : 1024 * MIXED].rearrange("p (u q v) -> p u q v", u=2, v=16)
                nc.vector.tensor_tensor(out=dst[:, :, 32 * lo : 32 * hi, :], in0=src, in1=src, op=ALU.mult)
            for b in chosen:
                if MIXED <= b < pre_banks(key[1]):
                    part = raw[key][:, 1024 * b : 1024 * b + 1024]
                    nc.vector.tensor_tensor(
                        out=squared[key][:, 1024 * b : 1024 * b + 1024], in0=part, in1=part, op=ALU.mult
                    )

        banks = {}

        def transposes(j):
            if j >= len(JOBS):
                return
            key = JOBS[j]
            words = raw[key][:].bitcast(F32)
            made = {}
            for b in range(4) if key[0] == "x" else BANK_ORDER:
                tp = tp_pool.tile([P, 4, P], F32, name="tp", tag="tp")
                for g in range(2):
                    for u in range(2):
                        col = 512 * b + 256 * g
                        if mixed_x(key):
                            col = 1024 * (b // 2) + 256 * (2 * g + b % 2)
                            region, src, order = 2 * g + u, words[:, col + u : col + 256 : 2], perm
                        elif key[0] == "a" and b < MIXED:
                            col = 512 * u + 128 * (2 * b + g)
                            region, order = 2 * u + g, ident
                            src = squared[key][:].bitcast(F32)[:, col : col + 128]
                        else:
                            region, order = 2 * u + g, ident
                            whole = words
                            if key[0] == "a" and b < pre_banks(key[1]):
                                whole = squared[key][:].bitcast(F32)
                            src = whole[:, col + u : col + 256 : 2]
                        nc.tensor.transpose(tp[:, region, :], src, order[:])
                made[b] = tp
            banks[key] = made

        w_raw = const.tile([P, 4, OUT_F], BF16, name="w_raw")
        bias_bf = const.tile([P, OUT_F], BF16, name="bias_bf")
        for j in range(A_BUFS):
            load(j)
            if j == 2:
                nc.sync.dma_start(out=w_raw[:].rearrange("p t c -> p (t c)"), in_=w_view)
            if j == 8:
                nc.sync.dma_start(out=bias_bf[:], in_=bias.partition_broadcast(P))

        w_grp = const.tile([P, OUT_F, 4], BF16, name="w_grp", align_bytes=64)
        w_codes = const.tile([P, OUT_F], U32, name="w_codes", align_bytes=64)
        w_scales = const.tile([P, OUT_F], U8, name="w_scales", align_bytes=64)
        sup_grp = const.tile([P, 8, OUT_F, 4], BF16, name="sup_grp", align_bytes=64)
        sup_codes = const.tile([P, 1024], U32, name="sup_codes", align_bytes=64)
        sup_scales = const.tile([P, 1024], U8, name="sup_scales", align_bytes=64)
        bias_f = const.tile([P, OUT_F], F32, name="bias_f")

        def weight_out():
            nc.vector.tensor_copy(out=w_grp[:], in_=w_raw[:].rearrange("p t c -> p c t"))

        def weight_quant():
            nc.vector.quantize_mx(
                out=w_codes[:].bitcast(FP8X4),
                scales=w_scales[:],
                in_=w_grp[:].rearrange("p c t -> p (c t)"),
            )

        grp = {}
        codes_of = {}

        def evacuate(j, chosen, copy):
            key = JOBS[j]
            if key not in grp:
                grp[key] = grp_pool.tile([P, 4096], BF16, name="grp", tag="grp", align_bytes=64)
            t = grp[key]
            for b, tp in banks[key].items():
                if b not in chosen:
                    continue
                halves = tp[:].rearrange("p (u g) c -> p u (g c)", u=2)
                if mixed_x(key):
                    dst = t[:].bitcast(F32).rearrange("p (n u e q j) -> p n e u q j", n=2, u=2, e=2, j=4)
                    copy(
                        out=dst[:, b // 2, b % 2],
                        in_=tp[:].rearrange("p j (u q) -> p u q j", u=2),
                    )
                elif key[0] == "x" or b < pre_banks(key[1]):
                    copy(
                        out=t[:].bitcast(F32)[:, 512 * b : 512 * b + 512].rearrange("p (c u) -> p c u", u=2),
                        in_=halves.rearrange("p u c -> p c u"),
                    )
                else:
                    nc.scalar.activation(
                        out=t[:, 1024 * b : 1024 * b + 1024].rearrange("p (c u e) -> p c u e", u=2, e=2),
                        in_=halves.bitcast(BF16).rearrange("p u (c e) -> p c u e", e=2),
                        func=ACT.Square,
                    )

        def quantise(j, lo=0, hi=4096):
            key = JOBS[j]
            if key not in codes_of:
                codes = q_pool.tile([P, 1024], U32, name="codes", tag="codes", align_bytes=64)
                scales = q_pool.tile([P, 1024], U8, name="scales", tag="scales", align_bytes=64)
                codes_of[key] = (codes, scales)
            codes, scales = codes_of[key]
            nc.vector.quantize_mx(
                out=codes[:, lo // 4 : hi // 4].bitcast(FP8X4),
                scales=scales[:, lo // 4 : hi // 4],
                in_=grp[key][:, lo:hi],
            )

        x_acc = {}

        def x_matmuls(h):
            codes, scales = codes_of[("x", h)]
            made = []
            for c in range(2):
                acc = acc_pool.tile([P, 4, OUT_F], F32, name="acc", tag="acc")
                for t in range(4):
                    cols = slice(512 * c + 128 * t, 512 * c + 128 * t + 128)
                    nc.tensor.matmul_mx(
                        out=acc[:, t, :],
                        lhsT=codes[:, cols].bitcast(FP8X4),
                        lhsT_scale=scales[:, cols],
                        rhs=w_codes[:].bitcast(FP8X4),
                        rhs_scale=w_scales[:],
                        start=True,
                        stop=True,
                    )
                made.append(acc)
            x_acc[h] = made

        def sup_out(h):
            for c in range(2):
                nc.scalar.copy(
                    out=sup_grp[:, 2 * h + c, :, :],
                    in_=x_acc[h][c][:].rearrange("p t w -> p w t"),
                )

        def sup_quant():
            nc.vector.quantize_mx(
                out=sup_codes[:].bitcast(FP8X4),
                scales=sup_scales[:],
                in_=sup_grp[:].rearrange("p c w t -> p (c w t)"),
            )

        units = [[4 * g, 4 * g + 1, 4 * g + 2, 4 * g + 3] for g in range(7)] + [[28, 29, 30], [31]]
        unit_of = {}
        for n, rows in enumerate(units):
            for i in rows:
                unit_of[i] = n
        unit_acc = {}
        unit_ep = {}

        def a_matmuls(i, g_lo=0, g_hi=8, first=0, final=7):
            n = unit_of[i]
            if n not in unit_acc:
                unit_acc[n] = acc_pool.tile([P, 4, OUT_F], F32, name="acc", tag="acc")
            acc = unit_acc[n]
            codes, scales = codes_of[("a", i)]
            s = i - units[n][0]
            for g in range(g_lo, g_hi):
                cols = slice(128 * g, 128 * g + 128)
                nc.tensor.matmul_mx(
                    out=acc[:, s, :],
                    lhsT=codes[:, cols].bitcast(FP8X4),
                    lhsT_scale=scales[:, cols],
                    rhs=sup_codes[:, cols].bitcast(FP8X4),
                    rhs_scale=sup_scales[:, cols],
                    start=(g == first),
                    stop=(g == final),
                )

        def ep_first(n):
            k = len(units[n])
            v = ep_pool.tile([P, 4, OUT_F], F32, name="v", tag="v")
            nc.vector.tensor_tensor(
                out=v[:, 0:k, :],
                in0=unit_acc[n][:, 0:k, :],
                in1=bias_f[:].unsqueeze(1).to_broadcast([P, k, OUT_F]),
                op=ALU.add,
            )
            unit_ep[n] = (v, None)

        def ep_min(n):
            k = len(units[n])
            v = unit_ep[n][0]
            m = ep_pool.tile([P, 4, OUT_F], F32, name="m", tag="m")
            nc.vector.tensor_scalar_min(out=m[:, 0:k, :], in0=v[:, 0:k, :], scalar1=0.0)
            unit_ep[n] = (v, m)

        def ep_exp(n):
            k = len(units[n])
            v, m = unit_ep[n]
            e = ep_pool.tile([P, 4, OUT_F], F32, name="e", tag="e")
            nc.scalar.activation(out=e[:, 0:k, :], in_=m[:, 0:k, :], func=ACT.Exp)
            unit_ep[n] = (v, e)

        def ep_last(n):
            k = len(units[n])
            v, e = unit_ep[n]
            o = ep_pool.tile([P, 4, OUT_F], F32, name="o", tag="o")
            nc.vector.scalar_tensor_tensor(
                out=o[:, 0:k, :],
                in0=e[:, 0:k, :],
                scalar=-1.0,
                in1=v[:, 0:k, :],
                op0=ALU.add,
                op1=ALU.max,
            )
            first = units[n][0]
            s0 = first % 4
            nc.sync.dma_start(out=out_view[first // 4][:, s0 : s0 + k, :], in_=o[:, 0:k, :])

        last = len(JOBS) - 1
        for lo in A0_CUTS[1:]:
            pre_square(0, (lo // 1024,))
        transposes(0)
        sup_ready = len(JOBS)
        ready = []
        todo = {}

        def plan(step, what, n):
            todo.setdefault((step, what), []).append(n)

        def due(step, what):
            return todo.pop((step, what), [])

        for j in range(last):
            for i in ready:
                if JOBS[i][0] == "x":
                    h = JOBS[i][1]
                    x_matmuls(h)
                    plan(j, "sup", h)
                    if h == X_TILES - 1:
                        plan(j + 1, "sup_quant", h)
            ready = [i for i in ready if JOBS[i][0] == "a"]
            if j >= sup_ready and j % 2 == 0:
                for i in ready[:4]:
                    r = JOBS[i][1]
                    a_matmuls(r)
                    n = unit_of[r]
                    if r == units[n][-1]:
                        plan(j, "first", n)
                        plan(j + 1, "exp", n)
                        plan(j + 2, "last", n)
                ready = ready[4:]
            if JOBS[j][0] == "x":
                evacuate(j, [b for b in range(4) if b not in X_VECTOR_BANKS], nc.scalar.copy)
                evacuate(j, X_VECTOR_BANKS, nc.vector.tensor_copy)
            else:
                evacuate(j, range(4), nc.scalar.copy)
            for n in due(j, "exp"):
                ep_exp(n)
            for n in due(j, "sup"):
                sup_out(n)
            for n in due(j, "last"):
                ep_last(n)
            if j == 2:
                weight_out()
            if j == 3:
                weight_quant()
            if j == 0 or j + 1 in LATE:
                pre_square(j + 1)
            transposes(j + 1)
            load(j + A_BUFS)
            if j >= LAG:
                quantise(j - LAG)
            for n in due(j, "first"):
                ep_first(n)
                plan(j, "min", n)
            if j + 2 not in LATE:
                pre_square(j + 2)
            for n in due(j, "min"):
                ep_min(n)
            if due(j, "sup_quant"):
                sup_quant()
                nc.vector.tensor_copy(out=bias_f[:], in_=bias_bf[:])
                sup_ready = j + 2
            if j >= LAG:
                ready.append(j - LAG)

        for n in due(last, "exp"):
            ep_exp(n)
        evacuate(last, [b for b in range(4) if b not in END_VECTOR_BANKS], nc.scalar.copy)
        for i in ready:
            a_matmuls(JOBS[i][1])
        quantise(last - 1)
        a_matmuls(TILES - 2)
        evacuate(last, END_VECTOR_BANKS, nc.vector.tensor_copy)
        for step in (last, last + 1):
            for n in due(step, "last"):
                ep_last(n)
        n = len(units) - 1
        for c, (lo, hi) in enumerate(END_CUTS):
            quantise(last, lo, hi)
            a_matmuls(TILES - 1, lo // 512, hi // 512, END_CUTS[0][0] // 512, END_CUTS[-1][1] // 512 - 1)
            if c == 0:
                ep_first(n - 1)
        ep_min(n - 1)
        ep_exp(n - 1)
        ep_first(n)
        ep_min(n)
        ep_exp(n)
        ep_last(n - 1)
        ep_last(n)
        assert not todo and len(ready) == 1
